import numpy as np
import ml_dtypes


def mxq(x, axis, fmt="e4m3"):
    dtype, down = {"e4m3": (ml_dtypes.float8_e4m3fn, 7), "e5m2": (ml_dtypes.float8_e5m2, 14)}[fmt]
    v = np.moveaxis(np.asarray(x, np.float32).astype(ml_dtypes.bfloat16).astype(np.float64), axis, -1)
    blocks = v.reshape(v.shape[:-1] + (-1, 32))
    amax = np.abs(blocks).max(-1, keepdims=True)
    byte = np.maximum(np.where(amax > 0, np.frexp(amax)[1] - 1 + 127, 0) - down, 1)
    scale = np.exp2(byte - 127.0)
    codes = (blocks / scale).astype(np.float32).astype(dtype).astype(np.float64)
    return np.moveaxis((codes * scale).reshape(v.shape), -1, axis)


WIDE = False


def mx_kscale(k):
    if not WIDE:
        return np.ones(k)
    levels = np.array([10, -10, 5, -5, 0])
    a = np.random.permutation(np.resize(levels, k // 512 * 4)).reshape(k // 512, 4)
    idx = np.arange(k)
    return np.exp2(a[idx // 512, idx % 128 // 32])


BF16 = ml_dtypes.bfloat16


def bf(x):
    return np.asarray(x, np.float32).astype(BF16)


def f64(x):
    return np.asarray(x).astype(np.float64)


E2M1 = np.array([0.0, 0.5, 1.0, 1.5, 2.0, 3.0, 4.0, 6.0, -0.0, -0.5, -1.0, -1.5, -2.0, -3.0, -4.0, -6.0])


def pack_weight(w, fmt):
    k, n = w.shape
    w = f64(bf(w)).reshape(k // 32, 32, n)
    amax = np.abs(w).max(1)
    if fmt == "e4m3":
        byte = np.frexp(amax)[1] - 1 + 127 - 7
    else:
        mant, ex = np.frexp(amax / 6.0)
        byte = np.where(mant > 0.5, ex, ex - 1) + 127
    byte = np.clip(np.where(amax > 0, byte, 1), 1, 254)
    scaled = (w * np.exp2(127.0 - byte)[:, None, :]).reshape(k, n).astype(np.float32)
    by_word = np.ascontiguousarray(scaled.reshape(k // 512, 128, 4, n).transpose(0, 1, 3, 2))
    if fmt == "e4m3":
        words = by_word.astype(ml_dtypes.float8_e4m3fn).view(np.uint8)
    else:
        c = by_word.astype(ml_dtypes.float4_e2m1fn).view(np.uint8) & 0xF
        words = c[..., 0::2] | (c[..., 1::2] << 4)
    return np.ascontiguousarray(words), np.ascontiguousarray(byte.astype(np.uint8).reshape(k // 512, 16, n))


def unpack_weight(words, scales, fmt):
    g, p, n, _ = words.shape
    if fmt == "e4m3":
        vals = np.ascontiguousarray(words).view(ml_dtypes.float8_e4m3fn).astype(np.float64)
    else:
        nib = np.empty((g, p, n, 4), np.uint8)
        nib[..., 0::2] = words & 0xF
        nib[..., 1::2] = words >> 4
        vals = E2M1[nib]
    vals = vals * np.repeat(np.exp2(scales.astype(np.float64) - 127.0), 8, axis=1)[..., None]
    return vals.transpose(0, 1, 3, 2).reshape(g * 512, n)


B, P, WS, D, H = 2, 64, 8, 512, 8
WN = P // WS
N = WS * WS
SHIFT = WS // 2
LN_EPS = 1e-5
FMT = "e4m3"


def layer_norm(x, g, b):
    mu = x.mean(-1, keepdims=True)
    var = x.var(-1, keepdims=True)
    return (x - mu) / np.sqrt(var + LN_EPS) * g + b


def window_merge(win):
    x = win.reshape(B, WN, WN, WS, WS, D).transpose(0, 1, 3, 2, 4, 5)
    return x.reshape(B, P, P, D)


def setup_inputs():
    s, t = mx_kscale(D), mx_kscale(D)
    x_mid = np.random.standard_normal((B, P * P, D)) * 1.4 + np.random.standard_normal((B, P * P, 1)) * 0.5
    attn_win = bf(np.random.standard_normal((B * WN * WN, N, D)) * 0.4 * s)
    x_mid = bf(x_mid)
    Wo2_words, Wo2_scales = pack_weight(np.random.standard_normal((D, D)) / np.sqrt(D) / s[:, None], FMT)
    bo2 = bf(0.1 * np.random.standard_normal(D))
    g4 = bf((1.0 + 0.1 * np.random.standard_normal(D)) * t)
    b4 = bf(0.1 * np.random.standard_normal(D) * t)
    Wl_words, Wl_scales = pack_weight(np.random.standard_normal((D, D)) / np.sqrt(D) / t[:, None], FMT)
    bl = bf(0.1 * np.random.standard_normal(D))
    return {"attn_win": attn_win,
            "x_mid": x_mid,
            "Wo2_words": Wo2_words,
            "Wo2_scales": Wo2_scales,
            "bo2": bo2,
            "g4": g4,
            "b4": b4,
            "Wl_words": Wl_words,
            "Wl_scales": Wl_scales,
            "bl": bl}


def reference(attn_win, x_mid, Wo2_words, Wo2_scales, bo2, g4, b4, Wl_words, Wl_scales, bl):
    a = (mxq(f64(attn_win), 2, "e4m3") @ unpack_weight(Wo2_words, Wo2_scales, FMT)) + f64(bo2)
    a = np.roll(window_merge(a), (-SHIFT, -SHIFT), axis=(1, 2)).reshape(B, P * P, D)
    x = f64(x_mid) + a
    h = layer_norm(x, f64(g4), f64(b4))
    return x + (mxq(h, 2, "e4m3") @ unpack_weight(Wl_words, Wl_scales, FMT)) + f64(bl)

@@ -1,0 +1,238 @@
+from contextlib import ExitStack
+
+import concourse.mybir as mybir
+from concourse.masks import make_identity
+
+FLOPS = 2 * 2 * 8192 * 512 * 512
+
+BF16 = mybir.dt.bfloat16
+F32 = mybir.dt.float32
+I32 = mybir.dt.int32
+U32 = mybir.dt.uint32
+U8 = mybir.dt.uint8
+FP8X4 = mybir.dt.float8_e4m3fn_x4
+ADD = mybir.AluOpType.add
+MULT = mybir.AluOpType.mult
+ACT = mybir.ActivationFunctionType
+
+P = 128
+D = 512
+PACK = 4
+SIDE = 64
+WINDOW = 8
+SHIFT = 4
+QUAD = 4
+GROUPS = SIDE // QUAD
+LN_EPS = 1e-5
+
+
+def load_weight(nc, pool, words, scales, label):
+    w_words = pool.tile([P, D], U32, name=label + "_words", align_bytes=64)
+    nc.sync.dma_start(out=w_words[:].bitcast(I32), in_=words.rearrange("o p n t -> (o p) (n t)").bitcast(I32))
+    w_plane = pool.tile([P, D], U8, name=label + "_plane", align_bytes=64)
+    nc.vector.memset(w_plane[:].bitcast(I32), 0)
+    for quadrant in range(4):
+        nc.sync.dma_start(
+            out=w_plane[32 * quadrant : 32 * quadrant + 4, :].bitcast(I32),
+            in_=scales[0, 4 * quadrant : 4 * quadrant + 4, :].bitcast(I32),
+        )
+    return w_words, w_plane
+
+
+def tile_successiveswintransfomerblock_pb_t_kernel(
+    tc, attn_win, x_mid, Wo2_words, Wo2_scales, bo2, g4, b4, Wl_words, Wl_scales, bl, out
+):
+    nc = tc.nc
+    attn_quads = attn_win.rearrange(
+        "(g wc) (i jh s) d -> wc jh g i (s d)", wc=WINDOW, i=WINDOW, jh=WINDOW // QUAD, s=QUAD
+    )
+    x_mid_quads = x_mid.rearrange("b (r m s) d -> m (b r) (s d)", r=SIDE, m=GROUPS, s=QUAD)
+    out_quads = out.rearrange("b (r m s) d -> m (b r) (s d)", r=SIDE, m=GROUPS, s=QUAD)
+
+    with ExitStack() as ctx:
+        const = ctx.enter_context(tc.tile_pool(name="const", bufs=1))
+        loads = ctx.enter_context(tc.tile_pool(name="loads", bufs=3))
+        work = ctx.enter_context(tc.tile_pool(name="work", bufs=2))
+        keep = ctx.enter_context(tc.tile_pool(name="keep", bufs=3))
+        psum_t = ctx.enter_context(tc.psum_pool(name="psum_t", bufs=1))
+        psum_mx = ctx.enter_context(tc.psum_pool(name="psum_mx", bufs=3))
+
+        wo_words, wo_plane = load_weight(nc, const, Wo2_words, Wo2_scales, "wo")
+        wl_words, wl_plane = load_weight(nc, const, Wl_words, Wl_scales, "wl")
+
+        bo2_rows = const.tile([P, D], BF16)
+        nc.scalar.dma_start(out=bo2_rows[:], in_=bo2.partition_broadcast(P))
+        bl_rows = const.tile([P, D], BF16)
+        nc.scalar.dma_start(out=bl_rows[:], in_=bl.partition_broadcast(P))
+        g_bf = const.tile([P, PACK], BF16)
+        nc.scalar.dma_start(out=g_bf[:], in_=g4.rearrange("(p t) -> p t", t=PACK))
+        b_bf = const.tile([P, PACK], BF16)
+        nc.scalar.dma_start(out=b_bf[:], in_=b4.rearrange("(p t) -> p t", t=PACK))
+        g_col = const.tile([P, PACK], F32)
+        nc.vector.tensor_copy(out=g_col[:], in_=g_bf[:])
+        b_col = const.tile([P, PACK], F32)
+        nc.vector.tensor_copy(out=b_col[:], in_=b_bf[:])
+
+        ident = const.tile([P, P], F32)
+        make_identity(nc, ident[:])
+        rot = const.tile([P, P], F32)
+        for image in range(P // SIDE):
+            lo = SIDE * image
+            nc.vector.tensor_copy(out=rot[:, lo : lo + SIDE - SHIFT], in_=ident[:, lo + SHIFT : lo + SIDE])
+            nc.vector.tensor_copy(out=rot[:, lo + SIDE - SHIFT : lo + SIDE], in_=ident[:, lo : lo + SHIFT])
+
+        live = {}
+
+        def front(group):
+            attn_sb = loads.tile([P, QUAD * D], BF16)
+            nc.sync.dma_start(out=attn_sb[:], in_=attn_quads[group // 2, group % 2])
+            xm_sb = loads.tile([P, QUAD, D], BF16)
+            nc.sync.dma_start(
+                out=xm_sb[:].rearrange("p s d -> p (s d)"), in_=x_mid_quads[(group - 1) % GROUPS]
+            )
+            c_sb = work.tile([P, QUAD, D], F32)
+            for s in range(QUAD):
+                nc.gpsimd.tensor_tensor(out=c_sb[:, s, :], in0=xm_sb[:, s, :], in1=bo2_rows[:], op=ADD)
+
+            attn_words = attn_sb[:].bitcast(F32)
+            a_grp = work.tile([P, QUAD * P * PACK], BF16, align_bytes=64)
+            a_grp_words = a_grp[:].bitcast(F32).rearrange("p (s k u) -> p s k u", s=QUAD, k=P, u=2)
+            for half in range(2):
+                attn_t = psum_t.tile([P, 2, 2, P], F32)
+                for s2 in range(2):
+                    s = 2 * half + s2
+                    for u in range(2):
+                        nc.tensor.transpose(
+                            attn_t[:, s2, u, :], attn_words[:, 256 * s + u : 256 * (s + 1) : 2], rot[:]
+                        )
+                nc.vector.tensor_copy(
+                    out=a_grp_words[:, 2 * half : 2 * half + 2], in_=attn_t[:].rearrange("p s u k -> p s k u")
+                )
+            a_codes = work.tile([P, QUAD * P], U32, align_bytes=64)
+            a_plane = work.tile([P, QUAD * P], U8, align_bytes=64)
+            nc.vector.quantize_mx(out=a_codes[:].bitcast(FP8X4), scales=a_plane[:], in_=a_grp[:])
+
+            x_sb = work.tile([P, QUAD, D], F32)
+            xb_sb = keep.tile([P, QUAD, D], F32)
+            row_sum = work.tile([P, QUAD], F32)
+            for s in range(QUAD):
+                cols = slice(P * s, P * (s + 1))
+                acc = psum_mx.tile([P, D], F32)
+                nc.tensor.matmul_mx(
+                    out=acc[:],
+                    lhsT=a_codes[:, cols].bitcast(FP8X4),
+                    lhsT_scale=a_plane[:, cols],
+                    rhs=wo_words[:].bitcast(FP8X4),
+                    rhs_scale=wo_plane[:],
+                    start=True,
+                    stop=True,
+                )
+                nc.vector.scalar_tensor_tensor(
+                    out=x_sb[:, s, :],
+                    in0=acc[:],
+                    scalar=1.0,
+                    in1=c_sb[:, s, :],
+                    op0=MULT,
+                    op1=ADD,
+                    accum_out=row_sum[:, s : s + 1],
+                )
+                nc.gpsimd.tensor_tensor(out=xb_sb[:, s, :], in0=x_sb[:, s, :], in1=bl_rows[:], op=ADD)
+            live[group] = {"x": x_sb, "xb": xb_sb, "row_sum": row_sum}
+
+        def middle(group):
+            x_sb = live[group]["x"]
+            neg_mean = work.tile([P, QUAD], F32)
+            nc.vector.tensor_scalar(
+                out=neg_mean[:], in0=live[group]["row_sum"][:], scalar1=-1.0 / D, scalar2=None, op0=MULT
+            )
+            sq_sum = work.tile([P, QUAD], F32)
+            for s in range(QUAD):
+                squares = work.tile([P, D], BF16)
+                nc.scalar.activation(
+                    out=squares[:],
+                    in_=x_sb[:, s, :],
+                    func=ACT.Square,
+                    bias=neg_mean[:, s : s + 1],
+                    scale=1.0,
+                    accum_out=sq_sum[:, s : s + 1],
+                )
+            std = work.tile([P, QUAD], F32)
+            nc.scalar.activation(out=std[:], in_=sq_sum[:], func=ACT.Sqrt, bias=eps_col[:], scale=1.0 / D)
+            rstd = work.tile([P, QUAD], F32)
+            nc.vector.reciprocal(out=rstd[:], in_=std[:])
+            shift = work.tile([P, QUAD], F32)
+            nc.vector.tensor_tensor(out=shift[:], in0=neg_mean[:], in1=rstd[:], op=MULT)
+            z_sb = work.tile([P, QUAD, PACK, P], F32)
+            for s in range(QUAD):
+                nc.scalar.activation(
+                    out=z_sb[:, s].rearrange("r t p -> r p t"),
+                    in_=x_sb[:, s, :].rearrange("r (p t) -> r p t", t=PACK),
+                    func=ACT.Identity,
+                    bias=shift[:, s : s + 1],
+                    scale=rstd[:, s : s + 1],
+                )
+            h_planes = work.tile([P, PACK, QUAD * P], BF16)
+            for t in range(PACK):
+                z_t = psum_t.tile([P, QUAD * P], F32, name="z_t%d" % t, tag="z_t%d" % t)
+                for s in range(QUAD):
+                    nc.tensor.transpose(z_t[:, P * s : P * (s + 1)], z_sb[:, s, t, :], ident[:])
+                if t % 2 == 0:
+                    nc.scalar.activation(
+                        out=h_planes[:, t, :],
+                        in_=z_t[:],
+                        func=ACT.Identity,
+                        bias=b_col[:, t : t + 1],
+                        scale=g_col[:, t : t + 1],
+                    )
+                else:
+                    nc.vector.tensor_scalar(
+                        out=h_planes[:, t, :],
+                        in0=z_t[:],
+                        scalar1=g_col[:, t : t + 1],
+                        scalar2=b_col[:, t : t + 1],
+                        op0=MULT,
+                        op1=ADD,
+                    )
+            h_grp = work.tile([P, QUAD * P, PACK], BF16, align_bytes=64)
+            nc.scalar.copy(
+                out=h_grp[:].rearrange("p (c i) t -> p c t i", i=4),
+                in_=h_planes[:].rearrange("p t (c i) -> p c t i", i=4),
+            )
+            h_codes = keep.tile([P, QUAD * P], U32, align_bytes=64)
+            h_plane = keep.tile([P, QUAD * P], U8, align_bytes=64)
+            nc.vector.quantize_mx(
+                out=h_codes[:].bitcast(FP8X4), scales=h_plane[:], in_=h_grp[:].rearrange("p k t -> p (k t)")
+            )
+            live[group]["h_codes"] = h_codes
+            live[group]["h_plane"] = h_plane
+
+        def back(group):
+            h_codes = live[group]["h_codes"]
+            h_plane = live[group]["h_plane"]
+            xb_sb = live[group]["xb"]
+            o_sb = work.tile([P, QUAD, D], F32)
+            for s in range(QUAD):
+                cols = slice(P * s, P * (s + 1))
+                acc = psum_mx.tile([P, D], F32)
+                nc.tensor.matmul_mx(
+                    out=acc[:],
+                    lhsT=h_codes[:, cols].bitcast(FP8X4),
+                    lhsT_scale=h_plane[:, cols],
+                    rhs=wl_words[:].bitcast(FP8X4),
+                    rhs_scale=wl_plane[:],
+                    start=True,
+                    stop=True,
+                )
+                nc.vector.tensor_tensor(out=o_sb[:, s, :], in0=acc[:], in1=xb_sb[:, s, :], op=ADD)
+            nc.sync.dma_start(out=out_quads[(group - 1) % GROUPS], in_=o_sb[:].rearrange("p s d -> p (s d)"))
+
+        eps_col = const.tile([P, 1], F32)
+        nc.vector.memset(eps_col[:], LN_EPS)
+
+        for step in range(GROUPS + 2):
+            if step < GROUPS:
+                front(step)
+            if 1 <= step <= GROUPS:
+                middle(step - 1)
+            if step >= 2:
+                back(step - 2)

@@ -91,8 +91,9 @@ def tile_successiveswintransfomerblock_pb_t_kernel(
                 out=xm_sb[:].rearrange("p s d -> p (s d)"), in_=x_mid_quads[(group - 1) % GROUPS]
             )
             c_sb = work.tile([P, QUAD, D], F32)
-            for s in range(QUAD):
-                nc.gpsimd.tensor_tensor(out=c_sb[:, s, :], in0=xm_sb[:, s, :], in1=bo2_rows[:], op=ADD)
+            nc.vector.tensor_tensor(
+                out=c_sb[:], in0=xm_sb[:], in1=bo2_rows[:].unsqueeze(1).to_broadcast([P, QUAD, D]), op=ADD
+            )
 
             attn_words = attn_sb[:].bitcast(F32)
             a_grp = work.tile([P, QUAD * P * PACK], BF16, align_bytes=64)
@@ -105,7 +106,7 @@ def tile_successiveswintransfomerblock_pb_t_kernel(
                         nc.tensor.transpose(
                             attn_t[:, s2, u, :], attn_words[:, 256 * s + u : 256 * (s + 1) : 2], rot[:]
                         )
-                nc.vector.tensor_copy(
+                nc.scalar.copy(
                     out=a_grp_words[:, 2 * half : 2 * half + 2], in_=attn_t[:].rearrange("p s u k -> p s k u")
                 )
             a_codes = work.tile([P, QUAD * P], U32, align_bytes=64)
@@ -136,7 +137,9 @@ def tile_successiveswintransfomerblock_pb_t_kernel(
                     op1=ADD,
                     accum_out=row_sum[:, s : s + 1],
                 )
-                nc.gpsimd.tensor_tensor(out=xb_sb[:, s, :], in0=x_sb[:, s, :], in1=bl_rows[:], op=ADD)
+            nc.vector.tensor_tensor(
+                out=xb_sb[:], in0=x_sb[:], in1=bl_rows[:].unsqueeze(1).to_broadcast([P, QUAD, D]), op=ADD
+            )
             live[group] = {"x": x_sb, "xb": xb_sb, "row_sum": row_sum}
 
         def middle(group):
@@ -176,23 +179,13 @@ def tile_successiveswintransfomerblock_pb_t_kernel(
                 z_t = psum_t.tile([P, QUAD * P], F32, name="z_t%d" % t, tag="z_t%d" % t)
                 for s in range(QUAD):
                     nc.tensor.transpose(z_t[:, P * s : P * (s + 1)], z_sb[:, s, t, :], ident[:])
-                if t % 2 == 0:
-                    nc.scalar.activation(
-                        out=h_planes[:, t, :],
-                        in_=z_t[:],
-                        func=ACT.Identity,
-                        bias=b_col[:, t : t + 1],
-                        scale=g_col[:, t : t + 1],
-                    )
-                else:
-                    nc.vector.tensor_scalar(
-                        out=h_planes[:, t, :],
-                        in0=z_t[:],
-                        scalar1=g_col[:, t : t + 1],
-                        scalar2=b_col[:, t : t + 1],
-                        op0=MULT,
-                        op1=ADD,
-                    )
+                nc.scalar.activation(
+                    out=h_planes[:, t, :],
+                    in_=z_t[:],
+                    func=ACT.Identity,
+                    bias=b_col[:, t : t + 1],
+                    scale=g_col[:, t : t + 1],
+                )
             h_grp = work.tile([P, QUAD * P, PACK], BF16, align_bytes=64)
             nc.scalar.copy(
                 out=h_grp[:].rearrange("p (c i) t -> p c t i", i=4),

@@ -179,13 +179,23 @@ def tile_successiveswintransfomerblock_pb_t_kernel(
                 z_t = psum_t.tile([P, QUAD * P], F32, name="z_t%d" % t, tag="z_t%d" % t)
                 for s in range(QUAD):
                     nc.tensor.transpose(z_t[:, P * s : P * (s + 1)], z_sb[:, s, t, :], ident[:])
-                nc.scalar.activation(
-                    out=h_planes[:, t, :],
-                    in_=z_t[:],
-                    func=ACT.Identity,
-                    bias=b_col[:, t : t + 1],
-                    scale=g_col[:, t : t + 1],
-                )
+                if t % 2 == 0:
+                    nc.scalar.activation(
+                        out=h_planes[:, t, :],
+                        in_=z_t[:],
+                        func=ACT.Identity,
+                        bias=b_col[:, t : t + 1],
+                        scale=g_col[:, t : t + 1],
+                    )
+                else:
+                    nc.vector.tensor_scalar(
+                        out=h_planes[:, t, :],
+                        in0=z_t[:],
+                        scalar1=g_col[:, t : t + 1],
+                        scalar2=b_col[:, t : t + 1],
+                        op0=MULT,
+                        op1=ADD,
+                    )
             h_grp = work.tile([P, QUAD * P, PACK], BF16, align_bytes=64)
             nc.scalar.copy(
                 out=h_grp[:].rearrange("p (c i) t -> p c t i", i=4),

@@ -90,10 +90,9 @@ def tile_successiveswintransfomerblock_pb_t_kernel(
             nc.sync.dma_start(
                 out=xm_sb[:].rearrange("p s d -> p (s d)"), in_=x_mid_quads[(group - 1) % GROUPS]
             )
-            c_sb = work.tile([P, QUAD, D], F32)
-            nc.vector.tensor_tensor(
-                out=c_sb[:], in0=xm_sb[:], in1=bo2_rows[:].unsqueeze(1).to_broadcast([P, QUAD, D]), op=ADD
-            )
+            c_sb = keep.tile([P, QUAD, D], F32)
+            for s in range(QUAD):
+                nc.gpsimd.tensor_tensor(out=c_sb[:, s, :], in0=xm_sb[:, s, :], in1=bo2_rows[:], op=ADD)
 
             attn_words = attn_sb[:].bitcast(F32)
             a_grp = work.tile([P, QUAD * P * PACK], BF16, align_bytes=64)

@@ -53,12 +53,32 @@ def tile_successiveswintransfomerblock_pb_t_kernel(
         const = ctx.enter_context(tc.tile_pool(name="const", bufs=1))
         loads = ctx.enter_context(tc.tile_pool(name="loads", bufs=3))
         work = ctx.enter_context(tc.tile_pool(name="work", bufs=2))
-        keep = ctx.enter_context(tc.tile_pool(name="keep", bufs=3))
-        psum_t = ctx.enter_context(tc.psum_pool(name="psum_t", bufs=1))
+        long_lived = ctx.enter_context(tc.tile_pool(name="long_lived", bufs=3))
+        stores = ctx.enter_context(tc.tile_pool(name="stores", bufs=4))
+        psum_attn = ctx.enter_context(tc.psum_pool(name="psum_attn", bufs=1))
+        psum_z = ctx.enter_context(tc.psum_pool(name="psum_z", bufs=1))
         psum_mx = ctx.enter_context(tc.psum_pool(name="psum_mx", bufs=3))
+        ctx.enter_context(tc.manual_schedule())
 
+        live = {}
+
+        def absent(group):
+            return not 0 <= group < GROUPS
+
+        def load(group):
+            if absent(group):
+                return
+            attn_sb = loads.tile([P, QUAD * D], BF16)
+            nc.sync.dma_start(out=attn_sb[:], in_=attn_quads[group // 2, group % 2])
+            xm_sb = loads.tile([P, QUAD, D], BF16)
+            nc.sync.dma_start(out=xm_sb[:].rearrange("p s d -> p (s d)"), in_=x_mid_quads[(group - 1) % GROUPS])
+            live[group] = {"attn": attn_sb, "xm": xm_sb}
+
+        load(0)
         wo_words, wo_plane = load_weight(nc, const, Wo2_words, Wo2_scales, "wo")
+        load(1)
         wl_words, wl_plane = load_weight(nc, const, Wl_words, Wl_scales, "wl")
+        load(2)
 
         bo2_rows = const.tile([P, D], BF16)
         nc.scalar.dma_start(out=bo2_rows[:], in_=bo2.partition_broadcast(P))
@@ -68,10 +88,6 @@ def tile_successiveswintransfomerblock_pb_t_kernel(
         nc.scalar.dma_start(out=g_bf[:], in_=g4.rearrange("(p t) -> p t", t=PACK))
         b_bf = const.tile([P, PACK], BF16)
         nc.scalar.dma_start(out=b_bf[:], in_=b4.rearrange("(p t) -> p t", t=PACK))
-        g_col = const.tile([P, PACK], F32)
-        nc.vector.tensor_copy(out=g_col[:], in_=g_bf[:])
-        b_col = const.tile([P, PACK], F32)
-        nc.vector.tensor_copy(out=b_col[:], in_=b_bf[:])
 
         ident = const.tile([P, P], F32)
         make_identity(nc, ident[:])
@@ -80,48 +96,70 @@ def tile_successiveswintransfomerblock_pb_t_kernel(
             lo = SIDE * image
             nc.vector.tensor_copy(out=rot[:, lo : lo + SIDE - SHIFT], in_=ident[:, lo + SHIFT : lo + SIDE])
             nc.vector.tensor_copy(out=rot[:, lo + SIDE - SHIFT : lo + SIDE], in_=ident[:, lo : lo + SHIFT])
+        g_col = const.tile([P, PACK], F32)
+        nc.vector.tensor_copy(out=g_col[:], in_=g_bf[:])
+        b_col = const.tile([P, PACK], F32)
+        nc.vector.tensor_copy(out=b_col[:], in_=b_bf[:])
+        eps_col = const.tile([P, 1], F32)
+        nc.vector.memset(eps_col[:], LN_EPS)
 
-        live = {}
-
-        def front(group):
-            attn_sb = loads.tile([P, QUAD * D], BF16)
-            nc.sync.dma_start(out=attn_sb[:], in_=attn_quads[group // 2, group % 2])
-            xm_sb = loads.tile([P, QUAD, D], BF16)
-            nc.sync.dma_start(
-                out=xm_sb[:].rearrange("p s d -> p (s d)"), in_=x_mid_quads[(group - 1) % GROUPS]
+        def add_bo2(group):
+            if absent(group):
+                return
+            c_sb = work.tile([P, QUAD, D], F32)
+            nc.vector.tensor_tensor(
+                out=c_sb[:],
+                in0=live[group]["xm"][:],
+                in1=bo2_rows[:].unsqueeze(1).to_broadcast([P, QUAD, D]),
+                op=ADD,
             )
-            c_sb = keep.tile([P, QUAD, D], F32)
-            for s in range(QUAD):
-                nc.gpsimd.tensor_tensor(out=c_sb[:, s, :], in0=xm_sb[:, s, :], in1=bo2_rows[:], op=ADD)
+            live[group]["c"] = c_sb
 
-            attn_words = attn_sb[:].bitcast(F32)
-            a_grp = work.tile([P, QUAD * P * PACK], BF16, align_bytes=64)
-            a_grp_words = a_grp[:].bitcast(F32).rearrange("p (s k u) -> p s k u", s=QUAD, k=P, u=2)
-            for half in range(2):
-                attn_t = psum_t.tile([P, 2, 2, P], F32)
-                for s2 in range(2):
-                    s = 2 * half + s2
-                    for u in range(2):
-                        nc.tensor.transpose(
-                            attn_t[:, s2, u, :], attn_words[:, 256 * s + u : 256 * (s + 1) : 2], rot[:]
-                        )
-                nc.scalar.copy(
-                    out=a_grp_words[:, 2 * half : 2 * half + 2], in_=attn_t[:].rearrange("p s u k -> p s k u")
-                )
+        def transpose_attn(group, half):
+            if absent(group):
+                return
+            attn_words = live[group]["attn"][:].bitcast(F32)
+            attn_t = psum_attn.tile([P, 2, 2, P], F32)
+            for s2 in range(2):
+                s = 2 * half + s2
+                for u in range(2):
+                    nc.tensor.transpose(attn_t[:, s2, u, :], attn_words[:, 256 * s + u : 256 * (s + 1) : 2], rot[:])
+            live[group]["attn_t"] = attn_t
+
+        def copy_attn(group, half):
+            if absent(group):
+                return
+            if half == 0:
+                a_grp = work.tile([P, QUAD * P * PACK], BF16, align_bytes=64)
+                live[group]["a_grp"] = a_grp
+            a_grp_words = live[group]["a_grp"][:].bitcast(F32).rearrange("p (s k u) -> p s k u", s=QUAD, k=P, u=2)
+            nc.scalar.copy(
+                out=a_grp_words[:, 2 * half : 2 * half + 2],
+                in_=live[group]["attn_t"][:].rearrange("p s u k -> p s k u"),
+            )
+
+        def quantise_attn(group):
+            if absent(group):
+                return
             a_codes = work.tile([P, QUAD * P], U32, align_bytes=64)
             a_plane = work.tile([P, QUAD * P], U8, align_bytes=64)
-            nc.vector.quantize_mx(out=a_codes[:].bitcast(FP8X4), scales=a_plane[:], in_=a_grp[:])
+            nc.vector.quantize_mx(out=a_codes[:].bitcast(FP8X4), scales=a_plane[:], in_=live[group]["a_grp"][:])
+            live[group]["a_codes"] = a_codes
+            live[group]["a_plane"] = a_plane
 
+        def project(group):
+            if absent(group):
+                return
+            tiles = live[group]
             x_sb = work.tile([P, QUAD, D], F32)
-            xb_sb = keep.tile([P, QUAD, D], F32)
-            row_sum = work.tile([P, QUAD], F32)
+            row_sum = long_lived.tile([P, QUAD], F32)
             for s in range(QUAD):
                 cols = slice(P * s, P * (s + 1))
                 acc = psum_mx.tile([P, D], F32)
                 nc.tensor.matmul_mx(
                     out=acc[:],
-                    lhsT=a_codes[:, cols].bitcast(FP8X4),
-                    lhsT_scale=a_plane[:, cols],
+                    lhsT=tiles["a_codes"][:, cols].bitcast(FP8X4),
+                    lhsT_scale=tiles["a_plane"][:, cols],
                     rhs=wo_words[:].bitcast(FP8X4),
                     rhs_scale=wo_plane[:],
                     start=True,
@@ -131,110 +169,150 @@ def tile_successiveswintransfomerblock_pb_t_kernel(
                     out=x_sb[:, s, :],
                     in0=acc[:],
                     scalar=1.0,
-                    in1=c_sb[:, s, :],
+                    in1=tiles["c"][:, s, :],
                     op0=MULT,
                     op1=ADD,
                     accum_out=row_sum[:, s : s + 1],
                 )
-            nc.vector.tensor_tensor(
-                out=xb_sb[:], in0=x_sb[:], in1=bl_rows[:].unsqueeze(1).to_broadcast([P, QUAD, D]), op=ADD
-            )
-            live[group] = {"x": x_sb, "xb": xb_sb, "row_sum": row_sum}
+            neg_mean = long_lived.tile([P, QUAD], F32)
+            nc.vector.tensor_scalar(out=neg_mean[:], in0=row_sum[:], scalar1=-1.0 / D, scalar2=None, op0=MULT)
+            tiles["x"] = x_sb
+            tiles["neg_mean"] = neg_mean
 
-        def middle(group):
-            x_sb = live[group]["x"]
-            neg_mean = work.tile([P, QUAD], F32)
-            nc.vector.tensor_scalar(
-                out=neg_mean[:], in0=live[group]["row_sum"][:], scalar1=-1.0 / D, scalar2=None, op0=MULT
+        def add_bl(group):
+            if absent(group):
+                return
+            xb_sb = long_lived.tile([P, QUAD, D], F32)
+            nc.vector.tensor_tensor(
+                out=xb_sb[:],
+                in0=live[group]["x"][:],
+                in1=bl_rows[:].unsqueeze(1).to_broadcast([P, QUAD, D]),
+                op=ADD,
             )
-            sq_sum = work.tile([P, QUAD], F32)
+            live[group]["xb"] = xb_sb
+
+        def sum_squares(group):
+            if absent(group):
+                return
+            tiles = live[group]
+            sq_sum = long_lived.tile([P, QUAD], F32)
             for s in range(QUAD):
                 squares = work.tile([P, D], BF16)
                 nc.scalar.activation(
                     out=squares[:],
-                    in_=x_sb[:, s, :],
+                    in_=tiles["x"][:, s, :],
                     func=ACT.Square,
-                    bias=neg_mean[:, s : s + 1],
+                    bias=tiles["neg_mean"][:, s : s + 1],
                     scale=1.0,
                     accum_out=sq_sum[:, s : s + 1],
                 )
-            std = work.tile([P, QUAD], F32)
+            std = long_lived.tile([P, QUAD], F32)
             nc.scalar.activation(out=std[:], in_=sq_sum[:], func=ACT.Sqrt, bias=eps_col[:], scale=1.0 / D)
-            rstd = work.tile([P, QUAD], F32)
-            nc.vector.reciprocal(out=rstd[:], in_=std[:])
-            shift = work.tile([P, QUAD], F32)
-            nc.vector.tensor_tensor(out=shift[:], in0=neg_mean[:], in1=rstd[:], op=MULT)
+            tiles["std"] = std
+
+        def inverse_std(group):
+            if absent(group):
+                return
+            tiles = live[group]
+            rstd = long_lived.tile([P, QUAD], F32)
+            nc.vector.reciprocal(out=rstd[:], in_=tiles["std"][:])
+            shift = long_lived.tile([P, QUAD], F32)
+            nc.vector.tensor_tensor(out=shift[:], in0=tiles["neg_mean"][:], in1=rstd[:], op=MULT)
+            tiles["rstd"] = rstd
+            tiles["shift"] = shift
+
+        def normalise(group):
+            if absent(group):
+                return
+            tiles = live[group]
             z_sb = work.tile([P, QUAD, PACK, P], F32)
             for s in range(QUAD):
                 nc.scalar.activation(
                     out=z_sb[:, s].rearrange("r t p -> r p t"),
-                    in_=x_sb[:, s, :].rearrange("r (p t) -> r p t", t=PACK),
+                    in_=tiles["x"][:, s, :].rearrange("r (p t) -> r p t", t=PACK),
                     func=ACT.Identity,
-                    bias=shift[:, s : s + 1],
-                    scale=rstd[:, s : s + 1],
+                    bias=tiles["shift"][:, s : s + 1],
+                    scale=tiles["rstd"][:, s : s + 1],
                 )
+            tiles["z"] = z_sb
+
+        def transpose_z(group):
+            if absent(group):
+                return
+            z_t = []
+            for t in range(PACK):
+                z_t.append(psum_z.tile([P, QUAD * P], F32, name="z_t%d" % t, tag="z_t%d" % t))
+            for s in range(QUAD):
+                for t in range(PACK):
+                    nc.tensor.transpose(z_t[t][:, P * s : P * (s + 1)], live[group]["z"][:, s, t, :], ident[:])
+            live[group]["z_t"] = z_t
+
+        def gain_and_bias(group):
+            if absent(group):
+                return
             h_planes = work.tile([P, PACK, QUAD * P], BF16)
             for t in range(PACK):
-                z_t = psum_t.tile([P, QUAD * P], F32, name="z_t%d" % t, tag="z_t%d" % t)
-                for s in range(QUAD):
-                    nc.tensor.transpose(z_t[:, P * s : P * (s + 1)], z_sb[:, s, t, :], ident[:])
-                if t % 2 == 0:
-                    nc.scalar.activation(
-                        out=h_planes[:, t, :],
-                        in_=z_t[:],
-                        func=ACT.Identity,
-                        bias=b_col[:, t : t + 1],
-                        scale=g_col[:, t : t + 1],
-                    )
-                else:
-                    nc.vector.tensor_scalar(
-                        out=h_planes[:, t, :],
-                        in0=z_t[:],
-                        scalar1=g_col[:, t : t + 1],
-                        scalar2=b_col[:, t : t + 1],
-                        op0=MULT,
-                        op1=ADD,
-                    )
+                nc.scalar.activation(
+                    out=h_planes[:, t, :],
+                    in_=live[group]["z_t"][t][:],
+                    func=ACT.Identity,
+                    bias=b_col[:, t : t + 1],
+                    scale=g_col[:, t : t + 1],
+                )
             h_grp = work.tile([P, QUAD * P, PACK], BF16, align_bytes=64)
             nc.scalar.copy(
                 out=h_grp[:].rearrange("p (c i) t -> p c t i", i=4),
                 in_=h_planes[:].rearrange("p t (c i) -> p c t i", i=4),
             )
-            h_codes = keep.tile([P, QUAD * P], U32, align_bytes=64)
-            h_plane = keep.tile([P, QUAD * P], U8, align_bytes=64)
+            live[group]["h_grp"] = h_grp
+
+        def quantise_h(group):
+            if absent(group):
+                return
+            h_codes = work.tile([P, QUAD * P], U32, align_bytes=64)
+            h_plane = work.tile([P, QUAD * P], U8, align_bytes=64)
             nc.vector.quantize_mx(
-                out=h_codes[:].bitcast(FP8X4), scales=h_plane[:], in_=h_grp[:].rearrange("p k t -> p (k t)")
+                out=h_codes[:].bitcast(FP8X4),
+                scales=h_plane[:],
+                in_=live[group]["h_grp"][:].rearrange("p k t -> p (k t)"),
             )
             live[group]["h_codes"] = h_codes
             live[group]["h_plane"] = h_plane
 
-        def back(group):
-            h_codes = live[group]["h_codes"]
-            h_plane = live[group]["h_plane"]
-            xb_sb = live[group]["xb"]
-            o_sb = work.tile([P, QUAD, D], F32)
+        def linear(group):
+            if absent(group):
+                return
+            tiles = live[group]
             for s in range(QUAD):
                 cols = slice(P * s, P * (s + 1))
                 acc = psum_mx.tile([P, D], F32)
                 nc.tensor.matmul_mx(
                     out=acc[:],
-                    lhsT=h_codes[:, cols].bitcast(FP8X4),
-                    lhsT_scale=h_plane[:, cols],
+                    lhsT=tiles["h_codes"][:, cols].bitcast(FP8X4),
+                    lhsT_scale=tiles["h_plane"][:, cols],
                     rhs=wl_words[:].bitcast(FP8X4),
                     rhs_scale=wl_plane[:],
                     start=True,
                     stop=True,
                 )
-                nc.vector.tensor_tensor(out=o_sb[:, s, :], in0=acc[:], in1=xb_sb[:, s, :], op=ADD)
-            nc.sync.dma_start(out=out_quads[(group - 1) % GROUPS], in_=o_sb[:].rearrange("p s d -> p (s d)"))
+                o_sb = stores.tile([P, D], F32)
+                nc.vector.tensor_tensor(out=o_sb[:], in0=acc[:], in1=tiles["xb"][:, s, :], op=ADD)
+                nc.sync.dma_start(out=out_quads[(group - 1) % GROUPS][:, D * s : D * (s + 1)], in_=o_sb[:])
 
-        eps_col = const.tile([P, 1], F32)
-        nc.vector.memset(eps_col[:], LN_EPS)
-
-        for step in range(GROUPS + 2):
-            if step < GROUPS:
-                front(step)
-            if 1 <= step <= GROUPS:
-                middle(step - 1)
-            if step >= 2:
-                back(step - 2)
+        for k in range(-2, GROUPS + 2):
+            load(k + 3) if k >= 0 else None
+            quantise_attn(k + 1)
+            add_bo2(k + 2)
+            sum_squares(k)
+            transpose_attn(k + 2, 0)
+            gain_and_bias(k - 1)
+            copy_attn(k + 2, 0)
+            inverse_std(k)
+            project(k + 1)
+            linear(k - 2)
+            quantise_h(k - 1)
+            add_bl(k)
+            normalise(k)
+            transpose_attn(k + 2, 1)
+            copy_attn(k + 2, 1)
+            transpose_z(k)

@@ -106,13 +106,9 @@ def tile_successiveswintransfomerblock_pb_t_kernel(
         def add_bo2(group):
             if absent(group):
                 return
-            c_sb = work.tile([P, QUAD, D], F32)
-            nc.vector.tensor_tensor(
-                out=c_sb[:],
-                in0=live[group]["xm"][:],
-                in1=bo2_rows[:].unsqueeze(1).to_broadcast([P, QUAD, D]),
-                op=ADD,
-            )
+            c_sb = long_lived.tile([P, QUAD, D], F32)
+            for s in range(QUAD):
+                nc.gpsimd.tensor_tensor(out=c_sb[:, s, :], in0=live[group]["xm"][:, s, :], in1=bo2_rows[:], op=ADD)
             live[group]["c"] = c_sb
 
         def transpose_attn(group, half):
@@ -252,13 +248,23 @@ def tile_successiveswintransfomerblock_pb_t_kernel(
                 return
             h_planes = work.tile([P, PACK, QUAD * P], BF16)
             for t in range(PACK):
-                nc.scalar.activation(
-                    out=h_planes[:, t, :],
-                    in_=live[group]["z_t"][t][:],
-                    func=ACT.Identity,
-                    bias=b_col[:, t : t + 1],
-                    scale=g_col[:, t : t + 1],
-                )
+                if t % 2 == 0:
+                    nc.scalar.activation(
+                        out=h_planes[:, t, :],
+                        in_=live[group]["z_t"][t][:],
+                        func=ACT.Identity,
+                        bias=b_col[:, t : t + 1],
+                        scale=g_col[:, t : t + 1],
+                    )
+                else:
+                    nc.vector.tensor_scalar(
+                        out=h_planes[:, t, :],
+                        in0=live[group]["z_t"][t][:],
+                        scalar1=g_col[:, t : t + 1],
+                        scalar2=b_col[:, t : t + 1],
+                        op0=MULT,
+                        op1=ADD,
+                    )
             h_grp = work.tile([P, QUAD * P, PACK], BF16, align_bytes=64)
             nc.scalar.copy(
                 out=h_grp[:].rearrange("p (c i) t -> p c t i", i=4),

@@ -171,7 +171,7 @@ def tile_successiveswintransfomerblock_pb_t_kernel(
                     accum_out=row_sum[:, s : s + 1],
                 )
             neg_mean = long_lived.tile([P, QUAD], F32)
-            nc.vector.tensor_scalar(out=neg_mean[:], in0=row_sum[:], scalar1=-1.0 / D, scalar2=None, op0=MULT)
+            nc.gpsimd.tensor_scalar(out=neg_mean[:], in0=row_sum[:], scalar1=-1.0 / D, scalar2=None, op0=MULT)
             tiles["x"] = x_sb
             tiles["neg_mean"] = neg_mean
 
@@ -213,7 +213,7 @@ def tile_successiveswintransfomerblock_pb_t_kernel(
             rstd = long_lived.tile([P, QUAD], F32)
             nc.vector.reciprocal(out=rstd[:], in_=tiles["std"][:])
             shift = long_lived.tile([P, QUAD], F32)
-            nc.vector.tensor_tensor(out=shift[:], in0=tiles["neg_mean"][:], in1=rstd[:], op=MULT)
+            nc.gpsimd.tensor_tensor(out=shift[:], in0=tiles["neg_mean"][:], in1=rstd[:], op=MULT)
             tiles["rstd"] = rstd
             tiles["shift"] = shift
 

@@ -24,6 +24,7 @@ SHIFT = 4
 QUAD = 4
 GROUPS = SIDE // QUAD
 LN_EPS = 1e-5
+GPSIMD_COLUMNS = 256
 
 
 def load_weight(nc, pool, words, scales, label):
@@ -57,7 +58,8 @@ def tile_successiveswintransfomerblock_pb_t_kernel(
         stores = ctx.enter_context(tc.tile_pool(name="stores", bufs=4))
         psum_attn = ctx.enter_context(tc.psum_pool(name="psum_attn", bufs=1))
         psum_z = ctx.enter_context(tc.psum_pool(name="psum_z", bufs=1))
-        psum_mx = ctx.enter_context(tc.psum_pool(name="psum_mx", bufs=3))
+        psum_mx = ctx.enter_context(tc.psum_pool(name="psum_mx", bufs=2))
+        psum_const = ctx.enter_context(tc.psum_pool(name="psum_const", bufs=1))
         ctx.enter_context(tc.manual_schedule())
 
         live = {}
@@ -78,7 +80,6 @@ def tile_successiveswintransfomerblock_pb_t_kernel(
         wo_words, wo_plane = load_weight(nc, const, Wo2_words, Wo2_scales, "wo")
         load(1)
         wl_words, wl_plane = load_weight(nc, const, Wl_words, Wl_scales, "wl")
-        load(2)
 
         bo2_rows = const.tile([P, D], BF16)
         nc.scalar.dma_start(out=bo2_rows[:], in_=bo2.partition_broadcast(P))
@@ -102,14 +103,21 @@ def tile_successiveswintransfomerblock_pb_t_kernel(
         nc.vector.tensor_copy(out=b_col[:], in_=b_bf[:])
         eps_col = const.tile([P, 1], F32)
         nc.vector.memset(eps_col[:], LN_EPS)
+        ident_bf = const.tile([P, P], BF16)
+        make_identity(nc, ident_bf[:])
+        bl_bank = psum_const.tile([P, D], F32)
+        nc.tensor.matmul(out=bl_bank[:], lhsT=ident_bf[:], rhs=bl_rows[:], start=True, stop=True)
 
-        def add_bo2(group):
+        def add_bo2(group, slots):
             if absent(group):
                 return
-            c_sb = long_lived.tile([P, QUAD, D], F32)
-            for s in range(QUAD):
-                nc.gpsimd.tensor_tensor(out=c_sb[:, s, :], in0=live[group]["xm"][:, s, :], in1=bo2_rows[:], op=ADD)
-            live[group]["c"] = c_sb
+            if 0 in slots:
+                c_sb = long_lived.tile([P, QUAD, D], F32)
+                live[group]["c"] = c_sb
+            for s in slots:
+                nc.gpsimd.tensor_tensor(
+                    out=live[group]["c"][:, s, :], in0=live[group]["xm"][:, s, :], in1=bo2_rows[:], op=ADD
+                )
 
         def transpose_attn(group, half):
             if absent(group):
@@ -170,10 +178,17 @@ def tile_successiveswintransfomerblock_pb_t_kernel(
                     op1=ADD,
                     accum_out=row_sum[:, s : s + 1],
                 )
-            neg_mean = long_lived.tile([P, QUAD], F32)
-            nc.gpsimd.tensor_scalar(out=neg_mean[:], in0=row_sum[:], scalar1=-1.0 / D, scalar2=None, op0=MULT)
             tiles["x"] = x_sb
-            tiles["neg_mean"] = neg_mean
+            tiles["row_sum"] = row_sum
+
+        def negative_mean(group):
+            if absent(group):
+                return
+            neg_mean = long_lived.tile([P, QUAD], F32)
+            nc.gpsimd.tensor_scalar(
+                out=neg_mean[:], in0=live[group]["row_sum"][:], scalar1=-1.0 / D, scalar2=None, op0=MULT
+            )
+            live[group]["neg_mean"] = neg_mean
 
         def add_bl(group):
             if absent(group):
@@ -182,7 +197,7 @@ def tile_successiveswintransfomerblock_pb_t_kernel(
             nc.vector.tensor_tensor(
                 out=xb_sb[:],
                 in0=live[group]["x"][:],
-                in1=bl_rows[:].unsqueeze(1).to_broadcast([P, QUAD, D]),
+                in1=bl_bank[:].unsqueeze(1).to_broadcast([P, QUAD, D]),
                 op=ADD,
             )
             live[group]["xb"] = xb_sb
@@ -209,13 +224,16 @@ def tile_successiveswintransfomerblock_pb_t_kernel(
         def inverse_std(group):
             if absent(group):
                 return
-            tiles = live[group]
             rstd = long_lived.tile([P, QUAD], F32)
-            nc.vector.reciprocal(out=rstd[:], in_=tiles["std"][:])
+            nc.vector.reciprocal(out=rstd[:], in_=live[group]["std"][:])
+            live[group]["rstd"] = rstd
+
+        def mean_over_std(group):
+            if absent(group):
+                return
             shift = long_lived.tile([P, QUAD], F32)
-            nc.gpsimd.tensor_tensor(out=shift[:], in0=tiles["neg_mean"][:], in1=rstd[:], op=MULT)
-            tiles["rstd"] = rstd
-            tiles["shift"] = shift
+            nc.gpsimd.tensor_tensor(out=shift[:], in0=live[group]["neg_mean"][:], in1=live[group]["rstd"][:], op=MULT)
+            live[group]["shift"] = shift
 
         def normalise(group):
             if absent(group):
@@ -248,29 +266,36 @@ def tile_successiveswintransfomerblock_pb_t_kernel(
                 return
             h_planes = work.tile([P, PACK, QUAD * P], BF16)
             for t in range(PACK):
-                if t % 2 == 0:
-                    nc.scalar.activation(
-                        out=h_planes[:, t, :],
-                        in_=live[group]["z_t"][t][:],
-                        func=ACT.Identity,
-                        bias=b_col[:, t : t + 1],
-                        scale=g_col[:, t : t + 1],
-                    )
-                else:
-                    nc.vector.tensor_scalar(
-                        out=h_planes[:, t, :],
-                        in0=live[group]["z_t"][t][:],
-                        scalar1=g_col[:, t : t + 1],
-                        scalar2=b_col[:, t : t + 1],
-                        op0=MULT,
-                        op1=ADD,
-                    )
+                nc.scalar.activation(
+                    out=h_planes[:, t, :],
+                    in_=live[group]["z_t"][t][:],
+                    func=ACT.Identity,
+                    bias=b_col[:, t : t + 1],
+                    scale=g_col[:, t : t + 1],
+                )
+            live[group]["h_planes"] = h_planes
+
+        def interleave_gpsimd(group):
+            if absent(group):
+                return
             h_grp = work.tile([P, QUAD * P, PACK], BF16, align_bytes=64)
-            nc.scalar.copy(
-                out=h_grp[:].rearrange("p (c i) t -> p c t i", i=4),
-                in_=h_planes[:].rearrange("p t (c i) -> p c t i", i=4),
+            nc.gpsimd.tensor_scalar(
+                out=h_grp[:, :GPSIMD_COLUMNS, :],
+                in0=live[group]["h_planes"][:, :, :GPSIMD_COLUMNS].rearrange("p t k -> p k t"),
+                scalar1=1.0,
+                scalar2=0.0,
+                op0=MULT,
+                op1=ADD,
             )
             live[group]["h_grp"] = h_grp
+
+        def interleave_vector(group):
+            if absent(group):
+                return
+            nc.vector.tensor_copy(
+                out=live[group]["h_grp"][:, GPSIMD_COLUMNS:, :],
+                in_=live[group]["h_planes"][:, :, GPSIMD_COLUMNS:].rearrange("p t k -> p k t"),
+            )
 
         def quantise_h(group):
             if absent(group):
@@ -305,20 +330,25 @@ def tile_successiveswintransfomerblock_pb_t_kernel(
                 nc.vector.tensor_tensor(out=o_sb[:], in0=acc[:], in1=tiles["xb"][:, s, :], op=ADD)
                 nc.sync.dma_start(out=out_quads[(group - 1) % GROUPS][:, D * s : D * (s + 1)], in_=o_sb[:])
 
-        for k in range(-2, GROUPS + 2):
-            load(k + 3) if k >= 0 else None
-            quantise_attn(k + 1)
-            add_bo2(k + 2)
-            sum_squares(k)
-            transpose_attn(k + 2, 0)
-            gain_and_bias(k - 1)
+        for k in range(-3, GROUPS + 2):
+            load(k + 3) if k + 3 >= 2 else None
             copy_attn(k + 2, 0)
+            interleave_vector(k - 2)
+            quantise_attn(k + 1)
+            quantise_h(k - 2)
             inverse_std(k)
-            project(k + 1)
-            linear(k - 2)
-            quantise_h(k - 1)
-            add_bl(k)
-            normalise(k)
+            mean_over_std(k)
             transpose_attn(k + 2, 1)
+            gain_and_bias(k - 1)
+            add_bo2(k + 2, (0, 1, 2))
+            project(k + 1)
+            negative_mean(k + 1)
+            add_bo2(k + 2, (3,))
             copy_attn(k + 2, 1)
+            normalise(k)
+            linear(k - 2)
+            interleave_gpsimd(k - 1)
+            add_bl(k)
             transpose_z(k)
+            sum_squares(k + 1)
+            transpose_attn(k + 3, 0)

@@ -24,7 +24,7 @@ SHIFT = 4
 QUAD = 4
 GROUPS = SIDE // QUAD
 LN_EPS = 1e-5
-GPSIMD_COLUMNS = 256
+SCALAR_COLUMNS = 192
 
 
 def load_weight(nc, pool, words, scales, label):
@@ -57,8 +57,8 @@ def tile_successiveswintransfomerblock_pb_t_kernel(
         long_lived = ctx.enter_context(tc.tile_pool(name="long_lived", bufs=3))
         stores = ctx.enter_context(tc.tile_pool(name="stores", bufs=4))
         psum_attn = ctx.enter_context(tc.psum_pool(name="psum_attn", bufs=1))
-        psum_z = ctx.enter_context(tc.psum_pool(name="psum_z", bufs=1))
-        psum_mx = ctx.enter_context(tc.psum_pool(name="psum_mx", bufs=2))
+        psum_z = ctx.enter_context(tc.psum_pool(name="psum_z", bufs=3))
+        psum_mx = ctx.enter_context(tc.psum_pool(name="psum_mx", bufs=3))
         psum_const = ctx.enter_context(tc.psum_pool(name="psum_const", bufs=1))
         ctx.enter_context(tc.manual_schedule())
 
@@ -151,13 +151,18 @@ def tile_successiveswintransfomerblock_pb_t_kernel(
             live[group]["a_codes"] = a_codes
             live[group]["a_plane"] = a_plane
 
-        def project(group):
+        def project(group, slots):
             if absent(group):
                 return
             tiles = live[group]
-            x_sb = work.tile([P, QUAD, D], F32)
-            row_sum = long_lived.tile([P, QUAD], F32)
-            for s in range(QUAD):
+            if 0 in slots:
+                x_new = work.tile([P, QUAD, D], F32, name="x_sb")
+                sum_new = long_lived.tile([P, QUAD], F32, name="row_sum")
+                tiles["x"] = x_new
+                tiles["row_sum"] = sum_new
+            x_sb = tiles["x"]
+            row_sum = tiles["row_sum"]
+            for s in slots:
                 cols = slice(P * s, P * (s + 1))
                 acc = psum_mx.tile([P, D], F32)
                 nc.tensor.matmul_mx(
@@ -178,8 +183,6 @@ def tile_successiveswintransfomerblock_pb_t_kernel(
                     op1=ADD,
                     accum_out=row_sum[:, s : s + 1],
                 )
-            tiles["x"] = x_sb
-            tiles["row_sum"] = row_sum
 
         def negative_mean(group):
             if absent(group):
@@ -250,42 +253,37 @@ def tile_successiveswintransfomerblock_pb_t_kernel(
                 )
             tiles["z"] = z_sb
 
-        def transpose_z(group):
+        def transpose_z(group, planes):
             if absent(group):
                 return
-            z_t = []
-            for t in range(PACK):
-                z_t.append(psum_z.tile([P, QUAD * P], F32, name="z_t%d" % t, tag="z_t%d" % t))
-            for s in range(QUAD):
-                for t in range(PACK):
-                    nc.tensor.transpose(z_t[t][:, P * s : P * (s + 1)], live[group]["z"][:, s, t, :], ident[:])
-            live[group]["z_t"] = z_t
+            for t in planes:
+                z_t = psum_z.tile([P, QUAD * P], F32)
+                for s in range(QUAD):
+                    nc.tensor.transpose(z_t[:, P * s : P * (s + 1)], live[group]["z"][:, s, t, :], ident[:])
+                live[group]["z_t%d" % t] = z_t
 
-        def gain_and_bias(group):
+        def gain_and_bias(group, planes):
             if absent(group):
                 return
-            h_planes = work.tile([P, PACK, QUAD * P], BF16)
-            for t in range(PACK):
+            if 0 in planes:
+                h_planes = work.tile([P, PACK, QUAD * P], BF16)
+                live[group]["h_planes"] = h_planes
+            for t in planes:
                 nc.scalar.activation(
-                    out=h_planes[:, t, :],
-                    in_=live[group]["z_t"][t][:],
+                    out=live[group]["h_planes"][:, t, :],
+                    in_=live[group]["z_t%d" % t][:],
                     func=ACT.Identity,
                     bias=b_col[:, t : t + 1],
                     scale=g_col[:, t : t + 1],
                 )
-            live[group]["h_planes"] = h_planes
 
-        def interleave_gpsimd(group):
+        def interleave_scalar(group):
             if absent(group):
                 return
             h_grp = work.tile([P, QUAD * P, PACK], BF16, align_bytes=64)
-            nc.gpsimd.tensor_scalar(
-                out=h_grp[:, :GPSIMD_COLUMNS, :],
-                in0=live[group]["h_planes"][:, :, :GPSIMD_COLUMNS].rearrange("p t k -> p k t"),
-                scalar1=1.0,
-                scalar2=0.0,
-                op0=MULT,
-                op1=ADD,
+            nc.scalar.copy(
+                out=h_grp[:, :SCALAR_COLUMNS, :].rearrange("p (c i) t -> p c t i", i=4),
+                in_=live[group]["h_planes"][:, :, :SCALAR_COLUMNS].rearrange("p t (c i) -> p c t i", i=4),
             )
             live[group]["h_grp"] = h_grp
 
@@ -293,8 +291,8 @@ def tile_successiveswintransfomerblock_pb_t_kernel(
             if absent(group):
                 return
             nc.vector.tensor_copy(
-                out=live[group]["h_grp"][:, GPSIMD_COLUMNS:, :],
-                in_=live[group]["h_planes"][:, :, GPSIMD_COLUMNS:].rearrange("p t k -> p k t"),
+                out=live[group]["h_grp"][:, SCALAR_COLUMNS:, :],
+                in_=live[group]["h_planes"][:, :, SCALAR_COLUMNS:].rearrange("p t k -> p k t"),
             )
 
         def quantise_h(group):
@@ -332,23 +330,26 @@ def tile_successiveswintransfomerblock_pb_t_kernel(
 
         for k in range(-3, GROUPS + 2):
             load(k + 3) if k + 3 >= 2 else None
-            copy_attn(k + 2, 0)
-            interleave_vector(k - 2)
-            quantise_attn(k + 1)
-            quantise_h(k - 2)
             inverse_std(k)
             mean_over_std(k)
-            transpose_attn(k + 2, 1)
-            gain_and_bias(k - 1)
-            add_bo2(k + 2, (0, 1, 2))
-            project(k + 1)
+            gain_and_bias(k - 1, (0,))
+            project(k + 1, (0, 1, 2))
+            transpose_z(k - 1, (3,))
+            project(k + 1, (3,))
+            gain_and_bias(k - 1, (1, 2, 3))
+            interleave_scalar(k - 1)
+            add_bo2(k + 2, (0, 1))
             negative_mean(k + 1)
-            add_bo2(k + 2, (3,))
-            copy_attn(k + 2, 1)
-            normalise(k)
+            add_bo2(k + 2, (2, 3))
+            copy_attn(k + 2, 0)
             linear(k - 2)
-            interleave_gpsimd(k - 1)
+            transpose_attn(k + 2, 1)
+            normalise(k)
+            copy_attn(k + 2, 1)
             add_bl(k)
-            transpose_z(k)
+            interleave_vector(k - 1)
+            quantise_attn(k + 2)
+            quantise_h(k - 1)
+            transpose_z(k, (0, 1, 2))
             sum_squares(k + 1)
             transpose_attn(k + 3, 0)

@@ -24,7 +24,7 @@ SHIFT = 4
 QUAD = 4
 GROUPS = SIDE // QUAD
 LN_EPS = 1e-5
-SCALAR_COLUMNS = 192
+SCALAR_COLUMNS = 128
 
 
 def load_weight(nc, pool, words, scales, label):
@@ -336,19 +336,20 @@ def tile_successiveswintransfomerblock_pb_t_kernel(
             project(k + 1, (0, 1, 2))
             transpose_z(k - 1, (3,))
             project(k + 1, (3,))
-            gain_and_bias(k - 1, (1, 2, 3))
+            gain_and_bias(k - 1, (1, 2))
+            copy_attn(k + 2, 0)
+            gain_and_bias(k - 1, (3,))
             interleave_scalar(k - 1)
             add_bo2(k + 2, (0, 1))
             negative_mean(k + 1)
             add_bo2(k + 2, (2, 3))
-            copy_attn(k + 2, 0)
             linear(k - 2)
             transpose_attn(k + 2, 1)
             normalise(k)
             copy_attn(k + 2, 1)
             add_bl(k)
-            interleave_vector(k - 1)
             quantise_attn(k + 2)
+            interleave_vector(k - 1)
             quantise_h(k - 1)
             transpose_z(k, (0, 1, 2))
             sum_squares(k + 1)

@@ -22,22 +22,26 @@ SIDE = 64
 WINDOW = 8
 SHIFT = 4
 QUAD = 4
-GROUPS = SIDE // QUAD
+QUADS = SIDE // QUAD
 LN_EPS = 1e-5
-SCALAR_COLUMNS = 128
+SIZES = (2, 2) + (4,) * 14 + (2, 2)
+SCALAR_SHARE = 4
+VECTOR_GROUPS = 2
+EARLY = 2
 
 
-def load_weight(nc, pool, words, scales, label):
+def load_words(nc, pool, words, label):
     w_words = pool.tile([P, D], U32, name=label + "_words", align_bytes=64)
     nc.sync.dma_start(out=w_words[:].bitcast(I32), in_=words.rearrange("o p n t -> (o p) (n t)").bitcast(I32))
-    w_plane = pool.tile([P, D], U8, name=label + "_plane", align_bytes=64)
-    nc.vector.memset(w_plane[:].bitcast(I32), 0)
+    return w_words
+
+
+def load_scales(nc, w_plane, scales):
     for quadrant in range(4):
         nc.sync.dma_start(
             out=w_plane[32 * quadrant : 32 * quadrant + 4, :].bitcast(I32),
             in_=scales[0, 4 * quadrant : 4 * quadrant + 4, :].bitcast(I32),
         )
-    return w_words, w_plane
 
 
 def tile_successiveswintransfomerblock_pb_t_kernel(
@@ -47,12 +51,12 @@ def tile_successiveswintransfomerblock_pb_t_kernel(
     attn_quads = attn_win.rearrange(
         "(g wc) (i jh s) d -> wc jh g i (s d)", wc=WINDOW, i=WINDOW, jh=WINDOW // QUAD, s=QUAD
     )
-    x_mid_quads = x_mid.rearrange("b (r m s) d -> m (b r) (s d)", r=SIDE, m=GROUPS, s=QUAD)
-    out_quads = out.rearrange("b (r m s) d -> m (b r) (s d)", r=SIDE, m=GROUPS, s=QUAD)
+    x_mid_quads = x_mid.rearrange("b (r m s) d -> m (b r) (s d)", r=SIDE, m=QUADS, s=QUAD)
+    out_quads = out.rearrange("b (r m s) d -> m (b r) (s d)", r=SIDE, m=QUADS, s=QUAD)
 
     with ExitStack() as ctx:
         const = ctx.enter_context(tc.tile_pool(name="const", bufs=1))
-        loads = ctx.enter_context(tc.tile_pool(name="loads", bufs=3))
+        loads = ctx.enter_context(tc.tile_pool(name="loads", bufs=4))
         work = ctx.enter_context(tc.tile_pool(name="work", bufs=2))
         long_lived = ctx.enter_context(tc.tile_pool(name="long_lived", bufs=3))
         stores = ctx.enter_context(tc.tile_pool(name="stores", bufs=4))
@@ -62,188 +66,215 @@ def tile_successiveswintransfomerblock_pb_t_kernel(
         psum_const = ctx.enter_context(tc.psum_pool(name="psum_const", bufs=1))
         ctx.enter_context(tc.manual_schedule())
 
-        live = {}
+        groups = []
+        taken = 0
+        for size in SIZES:
+            groups.append((taken // QUAD, taken % QUAD, size))
+            taken += size
+        live = [{} for _ in groups]
+        done = set()
 
-        def absent(group):
-            return not 0 <= group < GROUPS
+        def skip(name, group, part=0):
+            if not 0 <= group < len(groups) or (name, group, part) in done:
+                return True
+            done.add((name, group, part))
+            return False
 
-        def load(group):
-            if absent(group):
+        def load_attn(group):
+            if skip("load_attn", group):
                 return
+            quad, first, size = groups[group]
             attn_sb = loads.tile([P, QUAD * D], BF16)
-            nc.sync.dma_start(out=attn_sb[:], in_=attn_quads[group // 2, group % 2])
-            xm_sb = loads.tile([P, QUAD, D], BF16)
-            nc.sync.dma_start(out=xm_sb[:].rearrange("p s d -> p (s d)"), in_=x_mid_quads[(group - 1) % GROUPS])
-            live[group] = {"attn": attn_sb, "xm": xm_sb}
+            nc.sync.dma_start(
+                out=attn_sb[:, : D * size], in_=attn_quads[quad // 2, quad % 2][:, :, D * first : D * (first + size)]
+            )
+            live[group]["attn"] = attn_sb
 
-        load(0)
-        wo_words, wo_plane = load_weight(nc, const, Wo2_words, Wo2_scales, "wo")
-        load(1)
-        wl_words, wl_plane = load_weight(nc, const, Wl_words, Wl_scales, "wl")
-
-        bo2_rows = const.tile([P, D], BF16)
-        nc.scalar.dma_start(out=bo2_rows[:], in_=bo2.partition_broadcast(P))
-        bl_rows = const.tile([P, D], BF16)
-        nc.scalar.dma_start(out=bl_rows[:], in_=bl.partition_broadcast(P))
-        g_bf = const.tile([P, PACK], BF16)
-        nc.scalar.dma_start(out=g_bf[:], in_=g4.rearrange("(p t) -> p t", t=PACK))
-        b_bf = const.tile([P, PACK], BF16)
-        nc.scalar.dma_start(out=b_bf[:], in_=b4.rearrange("(p t) -> p t", t=PACK))
-
-        ident = const.tile([P, P], F32)
-        make_identity(nc, ident[:])
-        rot = const.tile([P, P], F32)
-        for image in range(P // SIDE):
-            lo = SIDE * image
-            nc.vector.tensor_copy(out=rot[:, lo : lo + SIDE - SHIFT], in_=ident[:, lo + SHIFT : lo + SIDE])
-            nc.vector.tensor_copy(out=rot[:, lo + SIDE - SHIFT : lo + SIDE], in_=ident[:, lo : lo + SHIFT])
-        g_col = const.tile([P, PACK], F32)
-        nc.vector.tensor_copy(out=g_col[:], in_=g_bf[:])
-        b_col = const.tile([P, PACK], F32)
-        nc.vector.tensor_copy(out=b_col[:], in_=b_bf[:])
-        eps_col = const.tile([P, 1], F32)
-        nc.vector.memset(eps_col[:], LN_EPS)
-        ident_bf = const.tile([P, P], BF16)
-        make_identity(nc, ident_bf[:])
-        bl_bank = psum_const.tile([P, D], F32)
-        nc.tensor.matmul(out=bl_bank[:], lhsT=ident_bf[:], rhs=bl_rows[:], start=True, stop=True)
-
-        def add_bo2(group, slots):
-            if absent(group):
+        def load_xm(group):
+            if skip("load_xm", group):
                 return
-            if 0 in slots:
-                c_sb = long_lived.tile([P, QUAD, D], F32)
-                live[group]["c"] = c_sb
+            quad, first, size = groups[group]
+            xm_sb = loads.tile([P, QUAD, D], BF16)
+            nc.sync.dma_start(
+                out=xm_sb[:, :size].rearrange("p s d -> p (s d)"),
+                in_=x_mid_quads[(quad - 1) % QUADS][:, D * first : D * (first + size)],
+            )
+            live[group]["xm"] = xm_sb
+
+        def add_bo2(group, slots=range(QUAD)):
             for s in slots:
-                nc.gpsimd.tensor_tensor(
-                    out=live[group]["c"][:, s, :], in0=live[group]["xm"][:, s, :], in1=bo2_rows[:], op=ADD
-                )
+                if 0 <= group < len(groups) and s >= groups[group][2]:
+                    continue
+                if skip("add_bo2", group, s):
+                    continue
+                if s == 0:
+                    c_sb = long_lived.tile([P, QUAD, D], F32)
+                    live[group]["c"] = c_sb
+                if group < VECTOR_GROUPS:
+                    nc.vector.tensor_tensor(
+                        out=live[group]["c"][:, s, :], in0=bo2_bank[:], in1=live[group]["xm"][:, s, :], op=ADD
+                    )
+                else:
+                    nc.gpsimd.tensor_tensor(
+                        out=live[group]["c"][:, s, :], in0=live[group]["xm"][:, s, :], in1=bo2_rows[:], op=ADD
+                    )
 
         def transpose_attn(group, half):
-            if absent(group):
+            if skip("transpose_attn", group, half) or 2 * half >= groups[group][2]:
                 return
             attn_words = live[group]["attn"][:].bitcast(F32)
-            attn_t = psum_attn.tile([P, 2, 2, P], F32)
-            for s2 in range(2):
+            if (group, half) in ((1, 0), (2, 0), (2, 1))[:EARLY]:
+                attn_t = psum_z.tile([P, 4 * P], F32, name="z_t")
+            else:
+                attn_t = psum_attn.tile([P, 4 * P], F32)
+            view = attn_t[:].rearrange("p (s u k) -> p s u k", s=2, u=2)
+            for s2 in range(min(2, groups[group][2] - 2 * half)):
                 s = 2 * half + s2
                 for u in range(2):
-                    nc.tensor.transpose(attn_t[:, s2, u, :], attn_words[:, 256 * s + u : 256 * (s + 1) : 2], rot[:])
-            live[group]["attn_t"] = attn_t
+                    nc.tensor.transpose(view[:, s2, u, :], attn_words[:, 256 * s + u : 256 * (s + 1) : 2], rot[:])
+            live[group]["attn_t%d" % half] = view
 
         def copy_attn(group, half):
-            if absent(group):
+            if skip("copy_attn", group, half) or 2 * half >= groups[group][2]:
                 return
             if half == 0:
                 a_grp = work.tile([P, QUAD * P * PACK], BF16, align_bytes=64)
                 live[group]["a_grp"] = a_grp
             a_grp_words = live[group]["a_grp"][:].bitcast(F32).rearrange("p (s k u) -> p s k u", s=QUAD, k=P, u=2)
+            width = min(2, groups[group][2] - 2 * half)
             nc.scalar.copy(
-                out=a_grp_words[:, 2 * half : 2 * half + 2],
-                in_=live[group]["attn_t"][:].rearrange("p s u k -> p s k u"),
+                out=a_grp_words[:, 2 * half : 2 * half + width],
+                in_=live[group]["attn_t%d" % half][:, :width].rearrange("p s u k -> p s k u"),
             )
 
         def quantise_attn(group):
-            if absent(group):
+            if skip("quantise_attn", group):
                 return
             a_codes = work.tile([P, QUAD * P], U32, align_bytes=64)
             a_plane = work.tile([P, QUAD * P], U8, align_bytes=64)
-            nc.vector.quantize_mx(out=a_codes[:].bitcast(FP8X4), scales=a_plane[:], in_=live[group]["a_grp"][:])
+            cols = groups[group][2] * P
+            nc.vector.quantize_mx(
+                out=a_codes[:, :cols].bitcast(FP8X4),
+                scales=a_plane[:, :cols],
+                in_=live[group]["a_grp"][:, : PACK * cols],
+            )
             live[group]["a_codes"] = a_codes
             live[group]["a_plane"] = a_plane
 
-        def project(group, slots):
-            if absent(group):
-                return
-            tiles = live[group]
-            if 0 in slots:
-                x_new = work.tile([P, QUAD, D], F32, name="x_sb")
-                sum_new = long_lived.tile([P, QUAD], F32, name="row_sum")
-                tiles["x"] = x_new
-                tiles["row_sum"] = sum_new
-            x_sb = tiles["x"]
-            row_sum = tiles["row_sum"]
+        def multiply(codes, plane, s, w_words, w_plane):
+            cols = slice(P * s, P * (s + 1))
+            acc = psum_mx.tile([P, D], F32)
+            nc.tensor.matmul_mx(
+                out=acc[:],
+                lhsT=codes[:, cols].bitcast(FP8X4),
+                lhsT_scale=plane[:, cols],
+                rhs=w_words[:].bitcast(FP8X4),
+                rhs_scale=w_plane[:],
+                start=True,
+                stop=True,
+            )
+            return acc
+
+        def project(group, slots=range(QUAD)):
             for s in slots:
-                cols = slice(P * s, P * (s + 1))
-                acc = psum_mx.tile([P, D], F32)
-                nc.tensor.matmul_mx(
-                    out=acc[:],
-                    lhsT=tiles["a_codes"][:, cols].bitcast(FP8X4),
-                    lhsT_scale=tiles["a_plane"][:, cols],
-                    rhs=wo_words[:].bitcast(FP8X4),
-                    rhs_scale=wo_plane[:],
-                    start=True,
-                    stop=True,
-                )
+                if 0 <= group < len(groups) and s >= groups[group][2]:
+                    continue
+                if skip("project", group, s):
+                    continue
+                tiles = live[group]
+                if s == 0:
+                    x_sb = work.tile([P, QUAD, D], F32)
+                    row_sum = long_lived.tile([P, QUAD], F32)
+                    tiles["x"] = x_sb
+                    tiles["row_sum"] = row_sum
+                acc = multiply(tiles["a_codes"], tiles["a_plane"], s, wo_words, wo_plane)
                 nc.vector.scalar_tensor_tensor(
-                    out=x_sb[:, s, :],
+                    out=tiles["x"][:, s, :],
                     in0=acc[:],
                     scalar=1.0,
                     in1=tiles["c"][:, s, :],
                     op0=MULT,
                     op1=ADD,
-                    accum_out=row_sum[:, s : s + 1],
+                    accum_out=tiles["row_sum"][:, s : s + 1],
                 )
 
-        def negative_mean(group):
-            if absent(group):
+        def negative_mean(group, part):
+            if skip("negative_mean", group, part):
                 return
-            neg_mean = long_lived.tile([P, QUAD], F32)
+            lo, hi = ((0, 1), (1, groups[group][2]))[part]
+            if lo == hi:
+                return
+            if part == 0:
+                neg_mean = long_lived.tile([P, QUAD], F32)
+                live[group]["neg_mean"] = neg_mean
             nc.gpsimd.tensor_scalar(
-                out=neg_mean[:], in0=live[group]["row_sum"][:], scalar1=-1.0 / D, scalar2=None, op0=MULT
+                out=live[group]["neg_mean"][:, lo:hi],
+                in0=live[group]["row_sum"][:, lo:hi],
+                scalar1=-1.0 / D,
+                scalar2=None,
+                op0=MULT,
             )
-            live[group]["neg_mean"] = neg_mean
 
         def add_bl(group):
-            if absent(group):
+            if skip("add_bl", group):
                 return
+            n = groups[group][2]
             xb_sb = long_lived.tile([P, QUAD, D], F32)
             nc.vector.tensor_tensor(
-                out=xb_sb[:],
-                in0=live[group]["x"][:],
-                in1=bl_bank[:].unsqueeze(1).to_broadcast([P, QUAD, D]),
+                out=xb_sb[:, :n],
+                in0=live[group]["x"][:, :n],
+                in1=bl_bank[:].unsqueeze(1).to_broadcast([P, n, D]),
                 op=ADD,
             )
             live[group]["xb"] = xb_sb
 
-        def sum_squares(group):
-            if absent(group):
-                return
-            tiles = live[group]
-            sq_sum = long_lived.tile([P, QUAD], F32)
-            for s in range(QUAD):
+        def sum_squares(group, slots=range(QUAD)):
+            for s in slots:
+                if 0 <= group < len(groups) and s >= groups[group][2]:
+                    continue
+                if skip("sum_squares", group, s):
+                    continue
+                tiles = live[group]
+                n = groups[group][2]
+                if s == 0:
+                    sq_sum = long_lived.tile([P, QUAD], F32)
+                    tiles["sq_sum"] = sq_sum
                 squares = work.tile([P, D], BF16)
                 nc.scalar.activation(
                     out=squares[:],
                     in_=tiles["x"][:, s, :],
                     func=ACT.Square,
-                    bias=tiles["neg_mean"][:, s : s + 1],
-                    scale=1.0,
-                    accum_out=sq_sum[:, s : s + 1],
+                    bias=tiles["row_sum"][:, s : s + 1],
+                    scale=-float(D),
+                    accum_out=tiles["sq_sum"][:, s : s + 1],
                 )
-            std = long_lived.tile([P, QUAD], F32)
-            nc.scalar.activation(out=std[:], in_=sq_sum[:], func=ACT.Sqrt, bias=eps_col[:], scale=1.0 / D)
-            tiles["std"] = std
-
-        def inverse_std(group):
-            if absent(group):
-                return
-            rstd = long_lived.tile([P, QUAD], F32)
-            nc.vector.reciprocal(out=rstd[:], in_=live[group]["std"][:])
-            live[group]["rstd"] = rstd
+                if s == n - 1:
+                    rstd = long_lived.tile([P, QUAD], F32)
+                    nc.scalar.activation(
+                        out=rstd[:, :n],
+                        in_=tiles["sq_sum"][:, :n],
+                        func=ACT.Abs_reciprocal_sqrt,
+                        bias=eps_col[:],
+                        scale=1.0 / D**3,
+                    )
+                    tiles["rstd"] = rstd
 
         def mean_over_std(group):
-            if absent(group):
+            if skip("mean_over_std", group):
                 return
+            n = groups[group][2]
             shift = long_lived.tile([P, QUAD], F32)
-            nc.gpsimd.tensor_tensor(out=shift[:], in0=live[group]["neg_mean"][:], in1=live[group]["rstd"][:], op=MULT)
+            nc.gpsimd.tensor_tensor(
+                out=shift[:, :n], in0=live[group]["neg_mean"][:, :n], in1=live[group]["rstd"][:, :n], op=MULT
+            )
             live[group]["shift"] = shift
 
         def normalise(group):
-            if absent(group):
+            if skip("normalise", group):
                 return
             tiles = live[group]
             z_sb = work.tile([P, QUAD, PACK, P], F32)
-            for s in range(QUAD):
+            for s in range(groups[group][2]):
                 nc.scalar.activation(
                     out=z_sb[:, s].rearrange("r t p -> r p t"),
                     in_=tiles["x"][:, s, :].rearrange("r (p t) -> r p t", t=PACK),
@@ -253,104 +284,214 @@ def tile_successiveswintransfomerblock_pb_t_kernel(
                 )
             tiles["z"] = z_sb
 
-        def transpose_z(group, planes):
-            if absent(group):
-                return
-            for t in planes:
-                z_t = psum_z.tile([P, QUAD * P], F32)
-                for s in range(QUAD):
-                    nc.tensor.transpose(z_t[:, P * s : P * (s + 1)], live[group]["z"][:, s, t, :], ident[:])
-                live[group]["z_t%d" % t] = z_t
+        def transpose_z(group, banks):
+            for bank in banks:
+                if skip("transpose_z", group, bank):
+                    continue
+                n = groups[group][2]
+                fit = QUAD // n
+                if bank * fit >= PACK:
+                    continue
+                z_t = psum_z.tile([P, 4 * P], F32)
+                view = z_t[:].rearrange("p (i s k) -> p i s k", i=fit, k=P)
+                for i in range(fit):
+                    for s in range(n):
+                        nc.tensor.transpose(view[:, i, s, :], live[group]["z"][:, s, bank * fit + i, :], ident[:])
+                live[group]["z_t%d" % bank] = z_t
 
-        def gain_and_bias(group, planes):
-            if absent(group):
-                return
-            if 0 in planes:
-                h_planes = work.tile([P, PACK, QUAD * P], BF16)
-                live[group]["h_planes"] = h_planes
-            for t in planes:
-                nc.scalar.activation(
-                    out=live[group]["h_planes"][:, t, :],
-                    in_=live[group]["z_t%d" % t][:],
-                    func=ACT.Identity,
-                    bias=b_col[:, t : t + 1],
-                    scale=g_col[:, t : t + 1],
-                )
+        def gain_and_bias(group, banks):
+            for bank in banks:
+                if skip("gain_and_bias", group, bank):
+                    continue
+                n = groups[group][2]
+                fit = QUAD // n
+                if bank * fit >= PACK:
+                    continue
+                if bank == 0:
+                    h_planes = work.tile([P, PACK, QUAD * P], BF16)
+                    live[group]["h_planes"] = h_planes
+                for i in range(fit):
+                    t = bank * fit + i
+                    nc.scalar.activation(
+                        out=live[group]["h_planes"][:, t, : n * P],
+                        in_=live[group]["z_t%d" % bank][:, n * P * i : n * P * (i + 1)],
+                        func=ACT.Identity,
+                        bias=b_col[:, t : t + 1],
+                        scale=g_col[:, t : t + 1],
+                    )
 
         def interleave_scalar(group):
-            if absent(group):
+            if skip("interleave_scalar", group):
                 return
             h_grp = work.tile([P, QUAD * P, PACK], BF16, align_bytes=64)
+            share = groups[group][2] * P // SCALAR_SHARE
             nc.scalar.copy(
-                out=h_grp[:, :SCALAR_COLUMNS, :].rearrange("p (c i) t -> p c t i", i=4),
-                in_=live[group]["h_planes"][:, :, :SCALAR_COLUMNS].rearrange("p t (c i) -> p c t i", i=4),
+                out=h_grp[:, :share, :].rearrange("p (c i) t -> p c t i", i=4),
+                in_=live[group]["h_planes"][:, :, :share].rearrange("p t (c i) -> p c t i", i=4),
             )
             live[group]["h_grp"] = h_grp
 
         def interleave_vector(group):
-            if absent(group):
+            if skip("interleave_vector", group):
                 return
+            cols = groups[group][2] * P
             nc.vector.tensor_copy(
-                out=live[group]["h_grp"][:, SCALAR_COLUMNS:, :],
-                in_=live[group]["h_planes"][:, :, SCALAR_COLUMNS:].rearrange("p t k -> p k t"),
+                out=live[group]["h_grp"][:, cols // SCALAR_SHARE : cols, :],
+                in_=live[group]["h_planes"][:, :, cols // SCALAR_SHARE : cols].rearrange("p t k -> p k t"),
             )
 
         def quantise_h(group):
-            if absent(group):
+            if skip("quantise_h", group):
                 return
             h_codes = work.tile([P, QUAD * P], U32, align_bytes=64)
             h_plane = work.tile([P, QUAD * P], U8, align_bytes=64)
+            cols = groups[group][2] * P
             nc.vector.quantize_mx(
-                out=h_codes[:].bitcast(FP8X4),
-                scales=h_plane[:],
-                in_=live[group]["h_grp"][:].rearrange("p k t -> p (k t)"),
+                out=h_codes[:, :cols].bitcast(FP8X4),
+                scales=h_plane[:, :cols],
+                in_=live[group]["h_grp"][:, :cols].rearrange("p k t -> p (k t)"),
             )
             live[group]["h_codes"] = h_codes
             live[group]["h_plane"] = h_plane
 
-        def linear(group):
-            if absent(group):
-                return
-            tiles = live[group]
-            for s in range(QUAD):
-                cols = slice(P * s, P * (s + 1))
-                acc = psum_mx.tile([P, D], F32)
-                nc.tensor.matmul_mx(
-                    out=acc[:],
-                    lhsT=tiles["h_codes"][:, cols].bitcast(FP8X4),
-                    lhsT_scale=tiles["h_plane"][:, cols],
-                    rhs=wl_words[:].bitcast(FP8X4),
-                    rhs_scale=wl_plane[:],
-                    start=True,
-                    stop=True,
-                )
+        def linear(group, slots=range(QUAD)):
+            for s in slots:
+                if 0 <= group < len(groups) and s >= groups[group][2]:
+                    continue
+                if skip("linear", group, s):
+                    continue
+                tiles = live[group]
+                quad, first, size = groups[group]
+                acc = multiply(tiles["h_codes"], tiles["h_plane"], s, wl_words, wl_plane)
                 o_sb = stores.tile([P, D], F32)
                 nc.vector.tensor_tensor(out=o_sb[:], in0=acc[:], in1=tiles["xb"][:, s, :], op=ADD)
-                nc.sync.dma_start(out=out_quads[(group - 1) % GROUPS][:, D * s : D * (s + 1)], in_=o_sb[:])
+                out_cols = slice(D * (first + s), D * (first + s + 1))
+                nc.sync.dma_start(out=out_quads[(quad - 1) % QUADS][:, out_cols], in_=o_sb[:])
 
-        for k in range(-3, GROUPS + 2):
-            load(k + 3) if k + 3 >= 2 else None
-            inverse_std(k)
-            mean_over_std(k)
-            gain_and_bias(k - 1, (0,))
-            project(k + 1, (0, 1, 2))
-            transpose_z(k - 1, (3,))
-            project(k + 1, (3,))
-            gain_and_bias(k - 1, (1, 2))
+        eps_col = const.tile([P, 1], F32)
+        nc.vector.memset(eps_col[:], LN_EPS)
+        warm = const.tile([P, 1], F32)
+        nc.scalar.activation(out=warm[:], in_=eps_col[:], func=ACT.Abs_reciprocal_sqrt, bias=0.0, scale=1.0)
+        wo_plane = const.tile([P, D], U8, align_bytes=64)
+        wl_plane = const.tile([P, D], U8, align_bytes=64)
+        bias_rows = const.tile([P, 2, D], BF16)
+        nc.vector.memset(bias_rows[:], 0.0)
+        nc.vector.memset(wo_plane[:].bitcast(I32), 0)
+        nc.vector.memset(wl_plane[:].bitcast(I32), 0)
+        ident = const.tile([P, P], F32)
+        make_identity(nc, ident[:])
+        ones = const.tile([P, P], BF16)
+        nc.gpsimd.memset(ones[:], 1.0)
+        rot = const.tile([P, P], F32)
+        for image in range(P // SIDE):
+            lo = SIDE * image
+            nc.vector.tensor_copy(out=rot[:, lo : lo + SIDE - SHIFT], in_=ident[:, lo + SHIFT : lo + SIDE])
+            nc.vector.tensor_copy(out=rot[:, lo + SIDE - SHIFT : lo + SIDE], in_=ident[:, lo : lo + SHIFT])
+        nc.scalar.dma_start(out=bias_rows[0:1, 0, :], in_=bo2.unsqueeze(0))
+        load_attn(0)
+        load_xm(0)
+        wo_words = load_words(nc, const, Wo2_words, "wo")
+        load_scales(nc, wo_plane, Wo2_scales)
+        load_attn(1)
+        nc.scalar.dma_start(out=bias_rows[0:1, 1, :], in_=bl.unsqueeze(0))
+        g_bf = const.tile([P, PACK], BF16)
+        nc.scalar.dma_start(out=g_bf[:], in_=g4.rearrange("(p t) -> p t", t=PACK))
+        b_bf = const.tile([P, PACK], BF16)
+        nc.scalar.dma_start(out=b_bf[:], in_=b4.rearrange("(p t) -> p t", t=PACK))
+        load_xm(1)
+        load_attn(2)
+        load_xm(2)
+        wl_words = load_words(nc, const, Wl_words, "wl")
+        load_scales(nc, wl_plane, Wl_scales)
+        load_attn(3)
+        load_xm(3)
+        transpose_attn(0, 0)
+        bo2_bank = psum_mx.tile([P, D], F32, name="acc")
+        nc.tensor.matmul(out=bo2_bank[:], lhsT=ones[:], rhs=bias_rows[:, 0, :], start=True, stop=True)
+        copy_attn(0, 0)
+        bo2_rows = const.tile([P, D], F32)
+        nc.scalar.copy(out=bo2_rows[:], in_=bo2_bank[:])
+        g_col = const.tile([P, PACK], F32)
+        nc.vector.tensor_copy(out=g_col[:], in_=g_bf[:])
+        b_col = const.tile([P, PACK], F32)
+        nc.vector.tensor_copy(out=b_col[:], in_=b_bf[:])
+        add_bo2(0)
+        quantise_attn(0)
+        transpose_attn(1, 0)
+        project(0)
+        bl_bank = psum_const.tile([P, D], F32)
+        nc.tensor.matmul(out=bl_bank[:], lhsT=ones[:], rhs=bias_rows[:, 1, :], start=True, stop=True)
+        copy_attn(1, 0)
+        add_bo2(1)
+        sum_squares(0)
+        negative_mean(0, 0)
+        negative_mean(0, 1)
+        load_attn(4)
+        load_xm(4)
+        transpose_attn(2, 0)
+        copy_attn(2, 0)
+        quantise_attn(1)
+        add_bl(0)
+        add_bo2(2, (0,))
+        mean_over_std(0)
+        add_bo2(2, (1, 2, 3))
+        transpose_attn(2, 1)
+        project(1)
+        copy_attn(2, 1)
+        normalise(0)
+        add_bl(1)
+        sum_squares(1)
+        negative_mean(1, 0)
+        negative_mean(1, 1)
+        mean_over_std(1)
+        quantise_attn(2)
+        transpose_z(0, (0, 1, 2))
+        gain_and_bias(0, (0, 1, 2, 3))
+        interleave_scalar(0)
+        project(2, (0, 1, 2))
+        interleave_vector(0)
+        transpose_attn(3, 0)
+        copy_attn(3, 0)
+        project(2, (3,))
+        quantise_h(0)
+        normalise(1)
+        add_bo2(3, (0, 1))
+        negative_mean(2, 0)
+        negative_mean(2, 1)
+        add_bo2(3, (2, 3))
+        transpose_attn(3, 1)
+        linear(0)
+        copy_attn(3, 1)
+        quantise_attn(3)
+        transpose_z(1, (0, 1, 2))
+        gain_and_bias(1, (0, 1, 2, 3))
+        interleave_scalar(1)
+        add_bl(2)
+
+        for k in range(-3, len(groups) + 2):
+            load_attn(k + 4)
+            load_xm(k + 3)
+            interleave_vector(k - 2)
+            quantise_h(k - 2)
+            quantise_attn(k + 1)
+            project(k, (0,))
+            negative_mean(k, 0)
+            add_bo2(k + 1)
+            project(k, (1, 2, 3))
+            negative_mean(k, 1)
+            add_bl(k - 1)
+            transpose_z(k - 1, (0, 1, 2))
             copy_attn(k + 2, 0)
-            gain_and_bias(k - 1, (3,))
-            interleave_scalar(k - 1)
-            add_bo2(k + 2, (0, 1))
-            negative_mean(k + 1)
-            add_bo2(k + 2, (2, 3))
-            linear(k - 2)
+            linear(k - 2, (0, 1))
+            sum_squares(k, (0, 1, 2))
+            gain_and_bias(k - 1, (0,))
+            sum_squares(k, (3,))
+            mean_over_std(k)
+            transpose_z(k - 1, (3,))
             transpose_attn(k + 2, 1)
-            normalise(k)
+            gain_and_bias(k - 1, (1, 2, 3))
+            linear(k - 2, (2, 3))
             copy_attn(k + 2, 1)
-            add_bl(k)
-            quantise_attn(k + 2)
-            interleave_vector(k - 1)
-            quantise_h(k - 1)
-            transpose_z(k, (0, 1, 2))
-            sum_squares(k + 1)
+            interleave_scalar(k - 1)
             transpose_attn(k + 3, 0)
+            normalise(k)

@@ -25,7 +25,9 @@ QUAD = 4
 QUADS = SIDE // QUAD
 LN_EPS = 1e-5
 SIZES = (2, 2) + (4,) * 14 + (2, 2)
-SCALAR_SHARE = 4
+VECTOR_COPIES = ()
+VECTOR_PLANES = ()
+SHARES = {}
 VECTOR_GROUPS = 2
 EARLY = 2
 
@@ -142,7 +144,8 @@ def tile_successiveswintransfomerblock_pb_t_kernel(
                 live[group]["a_grp"] = a_grp
             a_grp_words = live[group]["a_grp"][:].bitcast(F32).rearrange("p (s k u) -> p s k u", s=QUAD, k=P, u=2)
             width = min(2, groups[group][2] - 2 * half)
-            nc.scalar.copy(
+            copy = nc.vector.tensor_copy if (group, half) in VECTOR_COPIES else nc.scalar.copy
+            copy(
                 out=a_grp_words[:, 2 * half : 2 * half + width],
                 in_=live[group]["attn_t%d" % half][:, :width].rearrange("p s u k -> p s k u"),
             )
@@ -215,18 +218,20 @@ def tile_successiveswintransfomerblock_pb_t_kernel(
                 op0=MULT,
             )
 
-        def add_bl(group):
-            if skip("add_bl", group):
+        def add_bl(group, half):
+            if skip("add_bl", group, half):
                 return
             n = groups[group][2]
-            xb_sb = long_lived.tile([P, QUAD, D], F32)
+            lo, hi = half * n // 2, (half + 1) * n // 2
+            if half == 0:
+                xb_sb = long_lived.tile([P, QUAD, D], F32)
+                live[group]["xb"] = xb_sb
             nc.vector.tensor_tensor(
-                out=xb_sb[:, :n],
-                in0=live[group]["x"][:, :n],
-                in1=bl_bank[:].unsqueeze(1).to_broadcast([P, n, D]),
+                out=live[group]["xb"][:, lo:hi],
+                in0=live[group]["x"][:, lo:hi],
+                in1=bl_bank[:].unsqueeze(1).to_broadcast([P, hi - lo, D]),
                 op=ADD,
             )
-            live[group]["xb"] = xb_sb
 
         def sum_squares(group, slots=range(QUAD)):
             for s in slots:
@@ -312,6 +317,16 @@ def tile_successiveswintransfomerblock_pb_t_kernel(
                     live[group]["h_planes"] = h_planes
                 for i in range(fit):
                     t = bank * fit + i
+                    if (group, t) in VECTOR_PLANES:
+                        nc.vector.tensor_scalar(
+                            out=live[group]["h_planes"][:, t, : n * P],
+                            in0=live[group]["z_t%d" % bank][:, n * P * i : n * P * (i + 1)],
+                            scalar1=g_col[:, t : t + 1],
+                            scalar2=b_col[:, t : t + 1],
+                            op0=MULT,
+                            op1=ADD,
+                        )
+                        continue
                     nc.scalar.activation(
                         out=live[group]["h_planes"][:, t, : n * P],
                         in_=live[group]["z_t%d" % bank][:, n * P * i : n * P * (i + 1)],
@@ -320,11 +335,17 @@ def tile_successiveswintransfomerblock_pb_t_kernel(
                         scale=g_col[:, t : t + 1],
                     )
 
+        def scalar_share(group):
+            return int(groups[group][2] * P * SHARES.get(group, 0.25))
+
         def interleave_scalar(group):
             if skip("interleave_scalar", group):
                 return
             h_grp = work.tile([P, QUAD * P, PACK], BF16, align_bytes=64)
-            share = groups[group][2] * P // SCALAR_SHARE
+            share = scalar_share(group)
+            live[group]["h_grp"] = h_grp
+            if share == 0:
+                return
             nc.scalar.copy(
                 out=h_grp[:, :share, :].rearrange("p (c i) t -> p c t i", i=4),
                 in_=live[group]["h_planes"][:, :, :share].rearrange("p t (c i) -> p c t i", i=4),
@@ -335,9 +356,12 @@ def tile_successiveswintransfomerblock_pb_t_kernel(
             if skip("interleave_vector", group):
                 return
             cols = groups[group][2] * P
+            share = scalar_share(group)
+            if share == cols:
+                return
             nc.vector.tensor_copy(
-                out=live[group]["h_grp"][:, cols // SCALAR_SHARE : cols, :],
-                in_=live[group]["h_planes"][:, :, cols // SCALAR_SHARE : cols].rearrange("p t k -> p k t"),
+                out=live[group]["h_grp"][:, share:cols, :],
+                in_=live[group]["h_planes"][:, :, share:cols].rearrange("p t k -> p k t"),
             )
 
         def quantise_h(group):
@@ -389,17 +413,17 @@ def tile_successiveswintransfomerblock_pb_t_kernel(
             nc.vector.tensor_copy(out=rot[:, lo + SIDE - SHIFT : lo + SIDE], in_=ident[:, lo : lo + SHIFT])
         nc.scalar.dma_start(out=bias_rows[0:1, 0, :], in_=bo2.unsqueeze(0))
         load_attn(0)
-        load_xm(0)
         wo_words = load_words(nc, const, Wo2_words, "wo")
-        load_scales(nc, wo_plane, Wo2_scales)
         load_attn(1)
+        load_xm(0)
+        load_scales(nc, wo_plane, Wo2_scales)
         nc.scalar.dma_start(out=bias_rows[0:1, 1, :], in_=bl.unsqueeze(0))
         g_bf = const.tile([P, PACK], BF16)
         nc.scalar.dma_start(out=g_bf[:], in_=g4.rearrange("(p t) -> p t", t=PACK))
         b_bf = const.tile([P, PACK], BF16)
         nc.scalar.dma_start(out=b_bf[:], in_=b4.rearrange("(p t) -> p t", t=PACK))
-        load_xm(1)
         load_attn(2)
+        load_xm(1)
         load_xm(2)
         wl_words = load_words(nc, const, Wl_words, "wl")
         load_scales(nc, wl_plane, Wl_scales)
@@ -411,85 +435,108 @@ def tile_successiveswintransfomerblock_pb_t_kernel(
         copy_attn(0, 0)
         bo2_rows = const.tile([P, D], F32)
         nc.scalar.copy(out=bo2_rows[:], in_=bo2_bank[:])
+        transpose_attn(1, 0)
+        copy_attn(1, 0)
+        quantise_attn(0)
+        add_bo2(0)
+        quantise_attn(1)
+        project(0)
+        transpose_attn(2, 0)
+        copy_attn(2, 0)
+        transpose_attn(2, 1)
+        add_bo2(1)
+        load_attn(4)
+        load_xm(4)
+        sum_squares(0)
+        negative_mean(0, 0)
+        negative_mean(0, 1)
+        project(1)
+        copy_attn(2, 1)
+        bl_bank = psum_const.tile([P, D], F32)
+        nc.tensor.matmul(out=bl_bank[:], lhsT=ones[:], rhs=bias_rows[:, 1, :], start=True, stop=True)
+        add_bo2(2, (0,))
+        mean_over_std(0)
+        add_bo2(2, (1,))
+        quantise_attn(2)
         g_col = const.tile([P, PACK], F32)
         nc.vector.tensor_copy(out=g_col[:], in_=g_bf[:])
         b_col = const.tile([P, PACK], F32)
         nc.vector.tensor_copy(out=b_col[:], in_=b_bf[:])
-        add_bo2(0)
-        quantise_attn(0)
-        transpose_attn(1, 0)
-        project(0)
-        bl_bank = psum_const.tile([P, D], F32)
-        nc.tensor.matmul(out=bl_bank[:], lhsT=ones[:], rhs=bias_rows[:, 1, :], start=True, stop=True)
-        copy_attn(1, 0)
-        add_bo2(1)
-        sum_squares(0)
-        negative_mean(0, 0)
-        negative_mean(0, 1)
-        load_attn(4)
-        load_xm(4)
-        transpose_attn(2, 0)
-        copy_attn(2, 0)
-        quantise_attn(1)
-        add_bl(0)
-        add_bo2(2, (0,))
-        mean_over_std(0)
-        add_bo2(2, (1, 2, 3))
-        transpose_attn(2, 1)
-        project(1)
-        copy_attn(2, 1)
-        normalise(0)
-        add_bl(1)
         sum_squares(1)
+        normalise(0)
         negative_mean(1, 0)
         negative_mean(1, 1)
         mean_over_std(1)
-        quantise_attn(2)
+        add_bo2(2, (2, 3))
+        add_bl(0, 0)
+        add_bl(0, 1)
+        project(2, (0, 1))
+        transpose_attn(3, 0)
         transpose_z(0, (0, 1, 2))
+        copy_attn(3, 0)
+        add_bo2(3, (0, 1))
         gain_and_bias(0, (0, 1, 2, 3))
         interleave_scalar(0)
-        project(2, (0, 1, 2))
-        interleave_vector(0)
-        transpose_attn(3, 0)
-        copy_attn(3, 0)
-        project(2, (3,))
-        quantise_h(0)
+        project(2, (2, 3))
+        transpose_attn(3, 1)
+        add_bl(1, 0)
+        add_bl(1, 1)
         normalise(1)
-        add_bo2(3, (0, 1))
+        copy_attn(3, 1)
+        interleave_vector(0)
+        quantise_attn(3)
+        quantise_h(0)
         negative_mean(2, 0)
         negative_mean(2, 1)
         add_bo2(3, (2, 3))
-        transpose_attn(3, 1)
-        linear(0)
-        copy_attn(3, 1)
-        quantise_attn(3)
+        sum_squares(2)
+        mean_over_std(2)
+        load_attn(5)
+        load_xm(5)
+        project(3, (0, 1))
         transpose_z(1, (0, 1, 2))
+        transpose_attn(4, 0)
+        linear(0)
         gain_and_bias(1, (0, 1, 2, 3))
         interleave_scalar(1)
-        add_bl(2)
+        copy_attn(4, 0)
+        normalise(2)
+        transpose_attn(4, 1)
+        copy_attn(4, 1)
+        add_bl(2, 0)
+        project(3, (2, 3))
+        transpose_attn(5, 0)
+        interleave_vector(1)
+        quantise_attn(4)
+        quantise_h(1)
+        add_bl(2, 1)
+        load_attn(6)
+        load_xm(6)
 
         for k in range(-3, len(groups) + 2):
             load_attn(k + 4)
             load_xm(k + 3)
             interleave_vector(k - 2)
-            quantise_h(k - 2)
             quantise_attn(k + 1)
+            quantise_h(k - 2)
             project(k, (0,))
             negative_mean(k, 0)
             add_bo2(k + 1)
-            project(k, (1, 2, 3))
+            project(k, (1, 2))
+            add_bl(k - 1, 0)
+            project(k, (3,))
             negative_mean(k, 1)
-            add_bl(k - 1)
             transpose_z(k - 1, (0, 1, 2))
             copy_attn(k + 2, 0)
             linear(k - 2, (0, 1))
+            add_bl(k - 1, 1)
             sum_squares(k, (0, 1, 2))
-            gain_and_bias(k - 1, (0,))
+            gain_and_bias(k - 1, (0, 1))
             sum_squares(k, (3,))
             mean_over_std(k)
             transpose_z(k - 1, (3,))
             transpose_attn(k + 2, 1)
-            gain_and_bias(k - 1, (1, 2, 3))
+            gain_and_bias(k - 1, (2, 3))
             linear(k - 2, (2, 3))
             copy_attn(k + 2, 1)
             interleave_scalar(k - 1)

@@ -25,6 +25,12 @@ QUAD = 4
 QUADS = SIDE // QUAD
 LN_EPS = 1e-5
 SIZES = (2, 2) + (4,) * 14 + (2, 2)
+GP_COLS = 0
+WARM = 0
+WARM2 = 0
+REP_D = {}
+REP_K = {}
+PAIR = False
 VECTOR_COPIES = ()
 VECTOR_PLANES = ()
 SHARES = {}
@@ -121,6 +127,26 @@ def tile_successiveswintransfomerblock_pb_t_kernel(
                         out=live[group]["c"][:, s, :], in0=live[group]["xm"][:, s, :], in1=bo2_rows[:], op=ADD
                     )
 
+        def add_bo2_pairs(group):
+            for h in range(2):
+                if not 0 <= group < len(groups) or 2 * h >= groups[group][2]:
+                    continue
+                if ("add_bo2", group, 2 * h) in done:
+                    add_bo2(group, (2 * h, 2 * h + 1))
+                    continue
+                n2 = min(2, groups[group][2] - 2 * h)
+                for s in range(2 * h, 2 * h + n2):
+                    done.add(("add_bo2", group, s))
+                if h == 0:
+                    c_sb = long_lived.tile([P, QUAD, D], F32)
+                    live[group]["c"] = c_sb
+                nc.gpsimd.tensor_tensor(
+                    out=live[group]["c"][:, 2 * h : 2 * h + n2, :],
+                    in0=live[group]["xm"][:, 2 * h : 2 * h + n2, :],
+                    in1=bo2_rows[:].unsqueeze(1).to_broadcast([P, n2, D]),
+                    op=ADD,
+                )
+
         def transpose_attn(group, half):
             if skip("transpose_attn", group, half) or 2 * half >= groups[group][2]:
                 return
@@ -164,18 +190,19 @@ def tile_successiveswintransfomerblock_pb_t_kernel(
             live[group]["a_codes"] = a_codes
             live[group]["a_plane"] = a_plane
 
-        def multiply(codes, plane, s, w_words, w_plane):
+        def multiply(codes, plane, s, w_words, w_plane, repeats):
             cols = slice(P * s, P * (s + 1))
             acc = psum_mx.tile([P, D], F32)
-            nc.tensor.matmul_mx(
-                out=acc[:],
-                lhsT=codes[:, cols].bitcast(FP8X4),
-                lhsT_scale=plane[:, cols],
-                rhs=w_words[:].bitcast(FP8X4),
-                rhs_scale=w_plane[:],
-                start=True,
-                stop=True,
-            )
+            for repeat in range(repeats):
+                nc.tensor.matmul_mx(
+                    out=acc[:],
+                    lhsT=codes[:, cols].bitcast(FP8X4),
+                    lhsT_scale=plane[:, cols],
+                    rhs=w_words[:].bitcast(FP8X4),
+                    rhs_scale=w_plane[:],
+                    start=True,
+                    stop=True,
+                )
             return acc
 
         def project(group, slots=range(QUAD)):
@@ -190,7 +217,7 @@ def tile_successiveswintransfomerblock_pb_t_kernel(
                     row_sum = long_lived.tile([P, QUAD], F32)
                     tiles["x"] = x_sb
                     tiles["row_sum"] = row_sum
-                acc = multiply(tiles["a_codes"], tiles["a_plane"], s, wo_words, wo_plane)
+                acc = multiply(tiles["a_codes"], tiles["a_plane"], s, wo_words, wo_plane, REP_D.get(s, 1))
                 nc.vector.scalar_tensor_tensor(
                     out=tiles["x"][:, s, :],
                     in0=acc[:],
@@ -226,12 +253,41 @@ def tile_successiveswintransfomerblock_pb_t_kernel(
             if half == 0:
                 xb_sb = long_lived.tile([P, QUAD, D], F32)
                 live[group]["xb"] = xb_sb
+            if half == 1 and n == QUAD and GP_COLS:
+                flat = slice(2 * D, 4 * D - GP_COLS)
+                nc.vector.tensor_tensor(
+                    out=live[group]["xb"][:, 2, :], in0=live[group]["x"][:, 2, :], in1=bl_bank[:], op=ADD
+                )
+                if GP_COLS < D:
+                    nc.vector.tensor_tensor(
+                        out=live[group]["xb"][:, 3, : D - GP_COLS],
+                        in0=live[group]["x"][:, 3, : D - GP_COLS],
+                        in1=bl_bank[:, : D - GP_COLS],
+                        op=ADD,
+                    )
+                return
             nc.vector.tensor_tensor(
                 out=live[group]["xb"][:, lo:hi],
                 in0=live[group]["x"][:, lo:hi],
                 in1=bl_bank[:].unsqueeze(1).to_broadcast([P, hi - lo, D]),
                 op=ADD,
             )
+
+        def add_bl_gpsimd(group):
+            if GP_COLS == 0 or skip("add_bl_gpsimd", group) or groups[group][2] < QUAD:
+                return
+            nc.gpsimd.tensor_tensor(
+                out=live[group]["xb"][:, 3, D - GP_COLS :],
+                in0=live[group]["x"][:, 3, D - GP_COLS :],
+                in1=bl_rows[:, D - GP_COLS :],
+                op=ADD,
+            )
+
+        def keep_warm(group, count, part=0):
+            if count == 0 or group < 2 or skip("keep_warm", group, part):
+                return
+            for i in range(count):
+                nc.tensor.matmul(out=bl_bank[:], lhsT=ones[:], rhs=bias_rows[:, 1, :], start=True, stop=True)
 
         def sum_squares(group, slots=range(QUAD)):
             for s in slots:
@@ -386,7 +442,7 @@ def tile_successiveswintransfomerblock_pb_t_kernel(
                     continue
                 tiles = live[group]
                 quad, first, size = groups[group]
-                acc = multiply(tiles["h_codes"], tiles["h_plane"], s, wl_words, wl_plane)
+                acc = multiply(tiles["h_codes"], tiles["h_plane"], s, wl_words, wl_plane, REP_K.get(s, 1))
                 o_sb = stores.tile([P, D], F32)
                 nc.vector.tensor_tensor(out=o_sb[:], in0=acc[:], in1=tiles["xb"][:, s, :], op=ADD)
                 out_cols = slice(D * (first + s), D * (first + s + 1))
@@ -454,6 +510,8 @@ def tile_successiveswintransfomerblock_pb_t_kernel(
         copy_attn(2, 1)
         bl_bank = psum_const.tile([P, D], F32)
         nc.tensor.matmul(out=bl_bank[:], lhsT=ones[:], rhs=bias_rows[:, 1, :], start=True, stop=True)
+        bl_rows = const.tile([P, D], F32)
+        nc.vector.tensor_copy(out=bl_rows[:], in_=bl_bank[:])
         add_bo2(2, (0,))
         mean_over_std(0)
         add_bo2(2, (1,))
@@ -521,24 +579,29 @@ def tile_successiveswintransfomerblock_pb_t_kernel(
             quantise_h(k - 2)
             project(k, (0,))
             negative_mean(k, 0)
-            add_bo2(k + 1)
+            add_bo2_pairs(k + 1) if PAIR else add_bo2(k + 1)
             project(k, (1, 2))
             add_bl(k - 1, 0)
             project(k, (3,))
             negative_mean(k, 1)
-            transpose_z(k - 1, (0, 1, 2))
             copy_attn(k + 2, 0)
-            linear(k - 2, (0, 1))
-            add_bl(k - 1, 1)
             sum_squares(k, (0, 1, 2))
+            transpose_z(k - 1, (0, 1))
+            linear(k - 2, (0, 1))
+            transpose_z(k - 1, (2,))
+            transpose_attn(k + 2, 1)
+            add_bl(k - 1, 1)
             gain_and_bias(k - 1, (0, 1))
             sum_squares(k, (3,))
             mean_over_std(k)
+            add_bl_gpsimd(k - 1)
+            linear(k - 2, (2,))
             transpose_z(k - 1, (3,))
-            transpose_attn(k + 2, 1)
+            linear(k - 2, (3,))
             gain_and_bias(k - 1, (2, 3))
-            linear(k - 2, (2, 3))
             copy_attn(k + 2, 1)
             interleave_scalar(k - 1)
+            keep_warm(k, WARM)
             transpose_attn(k + 3, 0)
+            keep_warm(k, WARM2, 1)
             normalise(k)

@@ -25,12 +25,13 @@ QUAD = 4
 QUADS = SIDE // QUAD
 LN_EPS = 1e-5
 SIZES = (2, 2) + (4,) * 14 + (2, 2)
-GP_COLS = 0
+GP_COLS = 256
 WARM = 0
+HEAD_WARM = 0
 WARM2 = 0
 REP_D = {}
 REP_K = {}
-PAIR = False
+PAIR = True
 VECTOR_COPIES = ()
 VECTOR_PLANES = ()
 SHARES = {}
@@ -88,15 +89,20 @@ def tile_successiveswintransfomerblock_pb_t_kernel(
             done.add((name, group, part))
             return False
 
-        def load_attn(group):
-            if skip("load_attn", group):
+        def load_attn(group, half=None):
+            if half is None and skip("load_attn", group):
                 return
             quad, first, size = groups[group]
-            attn_sb = loads.tile([P, QUAD * D], BF16)
+            if half is None or half == 0:
+                attn_sb = loads.tile([P, QUAD * D], BF16)
+                live[group]["attn"] = attn_sb
+            lo, hi = (0, size) if half is None else (2 * half, 2 * half + 2)
+            if half == 1:
+                done.add(("load_attn", group, 0))
             nc.sync.dma_start(
-                out=attn_sb[:, : D * size], in_=attn_quads[quad // 2, quad % 2][:, :, D * first : D * (first + size)]
+                out=live[group]["attn"][:, D * lo : D * hi],
+                in_=attn_quads[quad // 2, quad % 2][:, :, D * (first + lo) : D * (first + hi)],
             )
-            live[group]["attn"] = attn_sb
 
         def load_xm(group):
             if skip("load_xm", group):
@@ -287,7 +293,7 @@ def tile_successiveswintransfomerblock_pb_t_kernel(
             if count == 0 or group < 2 or skip("keep_warm", group, part):
                 return
             for i in range(count):
-                nc.tensor.matmul(out=bl_bank[:], lhsT=ones[:], rhs=bias_rows[:, 1, :], start=True, stop=True)
+                nc.tensor.matmul(out=bl_bank[:], lhsT=ones[:, :P], rhs=bias_rows[:, 1, :], start=True, stop=True)
 
         def sum_squares(group, slots=range(QUAD)):
             for s in slots:
@@ -460,8 +466,11 @@ def tile_successiveswintransfomerblock_pb_t_kernel(
         nc.vector.memset(wl_plane[:].bitcast(I32), 0)
         ident = const.tile([P, P], F32)
         make_identity(nc, ident[:])
-        ones = const.tile([P, P], BF16)
+        ones = const.tile([P, D], BF16)
         nc.gpsimd.memset(ones[:], 1.0)
+        for i in range(HEAD_WARM):
+            acc = psum_mx.tile([P, D], F32)
+            nc.tensor.matmul(out=acc[:], lhsT=ones[:, :P], rhs=ones[:], start=True, stop=True)
         rot = const.tile([P, P], F32)
         for image in range(P // SIDE):
             lo = SIDE * image
@@ -478,16 +487,17 @@ def tile_successiveswintransfomerblock_pb_t_kernel(
         nc.scalar.dma_start(out=g_bf[:], in_=g4.rearrange("(p t) -> p t", t=PACK))
         b_bf = const.tile([P, PACK], BF16)
         nc.scalar.dma_start(out=b_bf[:], in_=b4.rearrange("(p t) -> p t", t=PACK))
-        load_attn(2)
+        load_attn(2, 0)
         load_xm(1)
+        load_attn(2, 1)
         load_xm(2)
         wl_words = load_words(nc, const, Wl_words, "wl")
         load_scales(nc, wl_plane, Wl_scales)
         load_attn(3)
         load_xm(3)
         transpose_attn(0, 0)
-        bo2_bank = psum_mx.tile([P, D], F32, name="acc")
-        nc.tensor.matmul(out=bo2_bank[:], lhsT=ones[:], rhs=bias_rows[:, 0, :], start=True, stop=True)
+        bo2_bank = psum_z.tile([P, D], F32, name="z_t")
+        nc.tensor.matmul(out=bo2_bank[:], lhsT=ones[:, :P], rhs=bias_rows[:, 0, :], start=True, stop=True)
         copy_attn(0, 0)
         bo2_rows = const.tile([P, D], F32)
         nc.scalar.copy(out=bo2_rows[:], in_=bo2_bank[:])
@@ -499,7 +509,6 @@ def tile_successiveswintransfomerblock_pb_t_kernel(
         project(0)
         transpose_attn(2, 0)
         copy_attn(2, 0)
-        transpose_attn(2, 1)
         add_bo2(1)
         load_attn(4)
         load_xm(4)
@@ -507,9 +516,10 @@ def tile_successiveswintransfomerblock_pb_t_kernel(
         negative_mean(0, 0)
         negative_mean(0, 1)
         project(1)
+        transpose_attn(2, 1)
         copy_attn(2, 1)
         bl_bank = psum_const.tile([P, D], F32)
-        nc.tensor.matmul(out=bl_bank[:], lhsT=ones[:], rhs=bias_rows[:, 1, :], start=True, stop=True)
+        nc.tensor.matmul(out=bl_bank[:], lhsT=ones[:, :P], rhs=bias_rows[:, 1, :], start=True, stop=True)
         bl_rows = const.tile([P, D], F32)
         nc.vector.tensor_copy(out=bl_rows[:], in_=bl_bank[:])
         add_bo2(2, (0,))
@@ -521,6 +531,7 @@ def tile_successiveswintransfomerblock_pb_t_kernel(
         b_col = const.tile([P, PACK], F32)
         nc.vector.tensor_copy(out=b_col[:], in_=b_bf[:])
         sum_squares(1)
+        transpose_attn(3, 0)
         normalise(0)
         negative_mean(1, 0)
         negative_mean(1, 1)
@@ -529,16 +540,15 @@ def tile_successiveswintransfomerblock_pb_t_kernel(
         add_bl(0, 0)
         add_bl(0, 1)
         project(2, (0, 1))
-        transpose_attn(3, 0)
         transpose_z(0, (0, 1, 2))
         copy_attn(3, 0)
         add_bo2(3, (0, 1))
         gain_and_bias(0, (0, 1, 2, 3))
         interleave_scalar(0)
-        project(2, (2, 3))
-        transpose_attn(3, 1)
         add_bl(1, 0)
         add_bl(1, 1)
+        project(2, (2, 3))
+        transpose_attn(3, 1)
         normalise(1)
         copy_attn(3, 1)
         interleave_vector(0)
@@ -551,8 +561,8 @@ def tile_successiveswintransfomerblock_pb_t_kernel(
         mean_over_std(2)
         load_attn(5)
         load_xm(5)
-        project(3, (0, 1))
         transpose_z(1, (0, 1, 2))
+        project(3, (0, 1))
         transpose_attn(4, 0)
         linear(0)
         gain_and_bias(1, (0, 1, 2, 3))
@@ -564,6 +574,7 @@ def tile_successiveswintransfomerblock_pb_t_kernel(
         add_bl(2, 0)
         project(3, (2, 3))
         transpose_attn(5, 0)
+        sum_squares(3, (0, 1, 2))
         interleave_vector(1)
         quantise_attn(4)
         quantise_h(1)

@@ -25,7 +25,7 @@ QUAD = 4
 QUADS = SIDE // QUAD
 LN_EPS = 1e-5
 SIZES = (2, 2) + (4,) * 14 + (2, 2)
-GP_COLS = 256
+GP_COLS = 0
 WARM = 0
 HEAD_WARM = 0
 WARM2 = 0
@@ -259,15 +259,14 @@ def tile_successiveswintransfomerblock_pb_t_kernel(
             if half == 0:
                 xb_sb = long_lived.tile([P, QUAD, D], F32)
                 live[group]["xb"] = xb_sb
-            if half == 1 and n == QUAD and GP_COLS:
-                flat = slice(2 * D, 4 * D - GP_COLS)
+            if half == 0 and n == QUAD and GP_COLS:
                 nc.vector.tensor_tensor(
-                    out=live[group]["xb"][:, 2, :], in0=live[group]["x"][:, 2, :], in1=bl_bank[:], op=ADD
+                    out=live[group]["xb"][:, 0, :], in0=live[group]["x"][:, 0, :], in1=bl_bank[:], op=ADD
                 )
                 if GP_COLS < D:
                     nc.vector.tensor_tensor(
-                        out=live[group]["xb"][:, 3, : D - GP_COLS],
-                        in0=live[group]["x"][:, 3, : D - GP_COLS],
+                        out=live[group]["xb"][:, 1, : D - GP_COLS],
+                        in0=live[group]["x"][:, 1, : D - GP_COLS],
                         in1=bl_bank[:, : D - GP_COLS],
                         op=ADD,
                     )
@@ -283,8 +282,8 @@ def tile_successiveswintransfomerblock_pb_t_kernel(
             if GP_COLS == 0 or skip("add_bl_gpsimd", group) or groups[group][2] < QUAD:
                 return
             nc.gpsimd.tensor_tensor(
-                out=live[group]["xb"][:, 3, D - GP_COLS :],
-                in0=live[group]["x"][:, 3, D - GP_COLS :],
+                out=live[group]["xb"][:, 1, D - GP_COLS :],
+                in0=live[group]["x"][:, 1, D - GP_COLS :],
                 in1=bl_rows[:, D - GP_COLS :],
                 op=ADD,
             )
@@ -600,7 +599,6 @@ def tile_successiveswintransfomerblock_pb_t_kernel(
             transpose_z(k - 1, (0, 1))
             linear(k - 2, (0, 1))
             transpose_z(k - 1, (2,))
-            transpose_attn(k + 2, 1)
             add_bl(k - 1, 1)
             gain_and_bias(k - 1, (0, 1))
             sum_squares(k, (3,))
@@ -608,6 +606,7 @@ def tile_successiveswintransfomerblock_pb_t_kernel(
             add_bl_gpsimd(k - 1)
             linear(k - 2, (2,))
             transpose_z(k - 1, (3,))
+            transpose_attn(k + 2, 1)
             linear(k - 2, (3,))
             gain_and_bias(k - 1, (2, 3))
             copy_attn(k + 2, 1)

@@ -24,14 +24,13 @@ SHIFT = 4
 QUAD = 4
 QUADS = SIDE // QUAD
 LN_EPS = 1e-5
-SIZES = (2, 2) + (4,) * 14 + (2, 2)
-GP_COLS = 0
+SIZES = (2, 2) + (4,) * 15
 WARM = 0
 HEAD_WARM = 0
 WARM2 = 0
 REP_D = {}
 REP_K = {}
-PAIR = True
+PAIR = False
 VECTOR_COPIES = ()
 VECTOR_PLANES = ()
 SHARES = {}
@@ -259,18 +258,6 @@ def tile_successiveswintransfomerblock_pb_t_kernel(
             if half == 0:
                 xb_sb = long_lived.tile([P, QUAD, D], F32)
                 live[group]["xb"] = xb_sb
-            if half == 0 and n == QUAD and GP_COLS:
-                nc.vector.tensor_tensor(
-                    out=live[group]["xb"][:, 0, :], in0=live[group]["x"][:, 0, :], in1=bl_bank[:], op=ADD
-                )
-                if GP_COLS < D:
-                    nc.vector.tensor_tensor(
-                        out=live[group]["xb"][:, 1, : D - GP_COLS],
-                        in0=live[group]["x"][:, 1, : D - GP_COLS],
-                        in1=bl_bank[:, : D - GP_COLS],
-                        op=ADD,
-                    )
-                return
             nc.vector.tensor_tensor(
                 out=live[group]["xb"][:, lo:hi],
                 in0=live[group]["x"][:, lo:hi],
@@ -278,21 +265,12 @@ def tile_successiveswintransfomerblock_pb_t_kernel(
                 op=ADD,
             )
 
-        def add_bl_gpsimd(group):
-            if GP_COLS == 0 or skip("add_bl_gpsimd", group) or groups[group][2] < QUAD:
+        def leave_port(group):
+            if not 3 <= group < len(groups) - 3 or ("leave_port", group) in done:
                 return
-            nc.gpsimd.tensor_tensor(
-                out=live[group]["xb"][:, 1, D - GP_COLS :],
-                in0=live[group]["x"][:, 1, D - GP_COLS :],
-                in1=bl_rows[:, D - GP_COLS :],
-                op=ADD,
-            )
-
-        def keep_warm(group, count, part=0):
-            if count == 0 or group < 2 or skip("keep_warm", group, part):
-                return
-            for i in range(count):
-                nc.tensor.matmul(out=bl_bank[:], lhsT=ones[:, :P], rhs=bias_rows[:, 1, :], start=True, stop=True)
+            done.add(("leave_port", group))
+            gate = work.tile([P, 32], U8)
+            nc.gpsimd.tensor_copy(out=gate[:], in_=live[group]["h_plane"][:, :32])
 
         def sum_squares(group, slots=range(QUAD)):
             for s in slots:
@@ -314,16 +292,20 @@ def tile_successiveswintransfomerblock_pb_t_kernel(
                     scale=-float(D),
                     accum_out=tiles["sq_sum"][:, s : s + 1],
                 )
-                if s == n - 1:
-                    rstd = long_lived.tile([P, QUAD], F32)
-                    nc.scalar.activation(
-                        out=rstd[:, :n],
-                        in_=tiles["sq_sum"][:, :n],
-                        func=ACT.Abs_reciprocal_sqrt,
-                        bias=eps_col[:],
-                        scale=1.0 / D**3,
-                    )
-                    tiles["rstd"] = rstd
+
+        def inverse_std(group):
+            if skip("inverse_std", group):
+                return
+            n = groups[group][2]
+            rstd = long_lived.tile([P, QUAD], F32)
+            nc.scalar.activation(
+                out=rstd[:, :n],
+                in_=live[group]["sq_sum"][:, :n],
+                func=ACT.Abs_reciprocal_sqrt,
+                bias=eps_col[:],
+                scale=1.0 / D**3,
+            )
+            live[group]["rstd"] = rstd
 
         def mean_over_std(group):
             if skip("mean_over_std", group):
@@ -397,7 +379,7 @@ def tile_successiveswintransfomerblock_pb_t_kernel(
                     )
 
         def scalar_share(group):
-            return int(groups[group][2] * P * SHARES.get(group, 0.25))
+            return int(groups[group][2] * P * SHARES.get(group, 0.3125))
 
         def interleave_scalar(group):
             if skip("interleave_scalar", group):
@@ -460,7 +442,7 @@ def tile_successiveswintransfomerblock_pb_t_kernel(
         wo_plane = const.tile([P, D], U8, align_bytes=64)
         wl_plane = const.tile([P, D], U8, align_bytes=64)
         bias_rows = const.tile([P, 2, D], BF16)
-        nc.vector.memset(bias_rows[:], 0.0)
+        nc.vector.memset(bias_rows[:].rearrange("p b n -> p (b n)").bitcast(I32), 0)
         nc.vector.memset(wo_plane[:].bitcast(I32), 0)
         nc.vector.memset(wl_plane[:].bitcast(I32), 0)
         ident = const.tile([P, P], F32)
@@ -477,23 +459,23 @@ def tile_successiveswintransfomerblock_pb_t_kernel(
             nc.vector.tensor_copy(out=rot[:, lo + SIDE - SHIFT : lo + SIDE], in_=ident[:, lo : lo + SHIFT])
         nc.scalar.dma_start(out=bias_rows[0:1, 0, :], in_=bo2.unsqueeze(0))
         load_attn(0)
-        wo_words = load_words(nc, const, Wo2_words, "wo")
+        load_scales(nc, wo_plane, Wo2_scales)
         load_attn(1)
         load_xm(0)
-        load_scales(nc, wo_plane, Wo2_scales)
-        nc.scalar.dma_start(out=bias_rows[0:1, 1, :], in_=bl.unsqueeze(0))
-        g_bf = const.tile([P, PACK], BF16)
-        nc.scalar.dma_start(out=g_bf[:], in_=g4.rearrange("(p t) -> p t", t=PACK))
-        b_bf = const.tile([P, PACK], BF16)
-        nc.scalar.dma_start(out=b_bf[:], in_=b4.rearrange("(p t) -> p t", t=PACK))
+        wo_words = load_words(nc, const, Wo2_words, "wo")
         load_attn(2, 0)
         load_xm(1)
         load_attn(2, 1)
         load_xm(2)
-        wl_words = load_words(nc, const, Wl_words, "wl")
-        load_scales(nc, wl_plane, Wl_scales)
+        nc.sync.dma_start(out=bias_rows[0:1, 1, :], in_=bl.unsqueeze(0))
+        g_bf = const.tile([P, PACK], BF16)
+        nc.sync.dma_start(out=g_bf[:], in_=g4.rearrange("(p t) -> p t", t=PACK))
+        b_bf = const.tile([P, PACK], BF16)
+        nc.sync.dma_start(out=b_bf[:], in_=b4.rearrange("(p t) -> p t", t=PACK))
         load_attn(3)
         load_xm(3)
+        wl_words = load_words(nc, const, Wl_words, "wl")
+        load_scales(nc, wl_plane, Wl_scales)
         transpose_attn(0, 0)
         bo2_bank = psum_z.tile([P, D], F32, name="z_t")
         nc.tensor.matmul(out=bo2_bank[:], lhsT=ones[:, :P], rhs=bias_rows[:, 0, :], start=True, stop=True)
@@ -519,9 +501,8 @@ def tile_successiveswintransfomerblock_pb_t_kernel(
         copy_attn(2, 1)
         bl_bank = psum_const.tile([P, D], F32)
         nc.tensor.matmul(out=bl_bank[:], lhsT=ones[:, :P], rhs=bias_rows[:, 1, :], start=True, stop=True)
-        bl_rows = const.tile([P, D], F32)
-        nc.vector.tensor_copy(out=bl_rows[:], in_=bl_bank[:])
         add_bo2(2, (0,))
+        inverse_std(0)
         mean_over_std(0)
         add_bo2(2, (1,))
         quantise_attn(2)
@@ -534,6 +515,7 @@ def tile_successiveswintransfomerblock_pb_t_kernel(
         normalise(0)
         negative_mean(1, 0)
         negative_mean(1, 1)
+        inverse_std(1)
         mean_over_std(1)
         add_bo2(2, (2, 3))
         add_bl(0, 0)
@@ -557,6 +539,7 @@ def tile_successiveswintransfomerblock_pb_t_kernel(
         negative_mean(2, 1)
         add_bo2(3, (2, 3))
         sum_squares(2)
+        inverse_std(2)
         mean_over_std(2)
         load_attn(5)
         load_xm(5)
@@ -602,16 +585,15 @@ def tile_successiveswintransfomerblock_pb_t_kernel(
             add_bl(k - 1, 1)
             gain_and_bias(k - 1, (0, 1))
             sum_squares(k, (3,))
+            gain_and_bias(k - 1, (2,))
+            inverse_std(k)
             mean_over_std(k)
-            add_bl_gpsimd(k - 1)
             linear(k - 2, (2,))
             transpose_z(k - 1, (3,))
             transpose_attn(k + 2, 1)
             linear(k - 2, (3,))
-            gain_and_bias(k - 1, (2, 3))
+            gain_and_bias(k - 1, (3,))
             copy_attn(k + 2, 1)
             interleave_scalar(k - 1)
-            keep_warm(k, WARM)
             transpose_attn(k + 3, 0)
-            keep_warm(k, WARM2, 1)
             normalise(k)

@@ -31,6 +31,7 @@ WARM2 = 0
 REP_D = {}
 REP_K = {}
 PAIR = False
+TAIL = True
 VECTOR_COPIES = ()
 VECTOR_PLANES = ()
 SHARES = {}
@@ -340,7 +341,10 @@ def tile_successiveswintransfomerblock_pb_t_kernel(
                 fit = QUAD // n
                 if bank * fit >= PACK:
                     continue
-                z_t = psum_z.tile([P, 4 * P], F32)
+                if TAIL and group == len(groups) - 1 and bank == 3:
+                    z_t = psum_attn.tile([P, 4 * P], F32, name="attn_t")
+                else:
+                    z_t = psum_z.tile([P, 4 * P], F32)
                 view = z_t[:].rearrange("p (i s k) -> p i s k", i=fit, k=P)
                 for i in range(fit):
                     for s in range(n):
@@ -387,6 +391,13 @@ def tile_successiveswintransfomerblock_pb_t_kernel(
             h_grp = work.tile([P, QUAD * P, PACK], BF16, align_bytes=64)
             share = scalar_share(group)
             live[group]["h_grp"] = h_grp
+            if group == len(groups) - 1 and TAIL:
+                cols = groups[group][2] * P
+                nc.scalar.copy(
+                    out=h_grp[:, cols // 2 : cols, :].rearrange("p (c i) t -> p c t i", i=4),
+                    in_=live[group]["h_planes"][:, :, cols // 2 : cols].rearrange("p t (c i) -> p c t i", i=4),
+                )
+                return
             if share == 0:
                 return
             nc.scalar.copy(
@@ -402,24 +413,30 @@ def tile_successiveswintransfomerblock_pb_t_kernel(
             share = scalar_share(group)
             if share == cols:
                 return
+            if group == len(groups) - 1 and TAIL:
+                share, cols = 0, cols // 2
             nc.vector.tensor_copy(
                 out=live[group]["h_grp"][:, share:cols, :],
                 in_=live[group]["h_planes"][:, :, share:cols].rearrange("p t k -> p k t"),
             )
 
-        def quantise_h(group):
-            if skip("quantise_h", group):
+        def quantise_h(group, half=0):
+            last = group == len(groups) - 1 and TAIL
+            if (half == 1 and not last) or skip("quantise_h", group, half):
                 return
-            h_codes = work.tile([P, QUAD * P], U32, align_bytes=64)
-            h_plane = work.tile([P, QUAD * P], U8, align_bytes=64)
+            if half == 0:
+                h_codes = work.tile([P, QUAD * P], U32, align_bytes=64)
+                h_plane = work.tile([P, QUAD * P], U8, align_bytes=64)
+                live[group]["h_codes"] = h_codes
+                live[group]["h_plane"] = h_plane
             cols = groups[group][2] * P
+            width = cols // 2 if last else cols
+            lo = half * width
             nc.vector.quantize_mx(
-                out=h_codes[:, :cols].bitcast(FP8X4),
-                scales=h_plane[:, :cols],
-                in_=live[group]["h_grp"][:, :cols].rearrange("p k t -> p (k t)"),
+                out=live[group]["h_codes"][:, lo : lo + width].bitcast(FP8X4),
+                scales=live[group]["h_plane"][:, lo : lo + width],
+                in_=live[group]["h_grp"][:, lo : lo + width].rearrange("p k t -> p (k t)"),
             )
-            live[group]["h_codes"] = h_codes
-            live[group]["h_plane"] = h_plane
 
         def linear(group, slots=range(QUAD)):
             for s in slots:
@@ -570,6 +587,7 @@ def tile_successiveswintransfomerblock_pb_t_kernel(
             interleave_vector(k - 2)
             quantise_attn(k + 1)
             quantise_h(k - 2)
+            quantise_h(k - 2, 1)
             project(k, (0,))
             negative_mean(k, 0)
             add_bo2_pairs(k + 1) if PAIR else add_bo2(k + 1)
@@ -579,9 +597,11 @@ def tile_successiveswintransfomerblock_pb_t_kernel(
             negative_mean(k, 1)
             copy_attn(k + 2, 0)
             sum_squares(k, (0, 1, 2))
+            if k >= len(groups):
+                linear(k - 2, (0, 1))
             transpose_z(k - 1, (0, 1))
             linear(k - 2, (0, 1))
-            transpose_z(k - 1, (2,))
+            transpose_z(k - 1, (2,) if k < len(groups) else (2, 3))
             add_bl(k - 1, 1)
             gain_and_bias(k - 1, (0, 1))
             sum_squares(k, (3,))

@@ -32,6 +32,14 @@ REP_D = {}
 REP_K = {}
 PAIR = False
 TAIL = True
+JOINT = True
+PE_SLOTS = ()
+FIRST_PE = 3
+LAST_PE = 1
+DIAG_ENGINE = "scalar"
+G_COLS = 0
+FIRST_G = 2
+TAIL_WARM = 0
 VECTOR_COPIES = ()
 VECTOR_PLANES = ()
 SHARES = {}
@@ -83,6 +91,9 @@ def tile_successiveswintransfomerblock_pb_t_kernel(
         live = [{} for _ in groups]
         done = set()
 
+        def joint(group):
+            return JOINT and 5 <= group < len(groups)
+
         def skip(name, group, part=0):
             if not 0 <= group < len(groups) or (name, group, part) in done:
                 return True
@@ -104,12 +115,12 @@ def tile_successiveswintransfomerblock_pb_t_kernel(
                 in_=attn_quads[quad // 2, quad % 2][:, :, D * (first + lo) : D * (first + hi)],
             )
 
-        def load_xm(group):
+        def load_xm(group, queue=nc.sync):
             if skip("load_xm", group):
                 return
             quad, first, size = groups[group]
             xm_sb = loads.tile([P, QUAD, D], BF16)
-            nc.sync.dma_start(
+            queue.dma_start(
                 out=xm_sb[:, :size].rearrange("p s d -> p (s d)"),
                 in_=x_mid_quads[(quad - 1) % QUADS][:, D * first : D * (first + size)],
             )
@@ -172,9 +183,15 @@ def tile_successiveswintransfomerblock_pb_t_kernel(
             if skip("copy_attn", group, half) or 2 * half >= groups[group][2]:
                 return
             if half == 0:
-                a_grp = work.tile([P, QUAD * P * PACK], BF16, align_bytes=64)
-                live[group]["a_grp"] = a_grp
-            a_grp_words = live[group]["a_grp"][:].bitcast(F32).rearrange("p (s k u) -> p s k u", s=QUAD, k=P, u=2)
+                if joint(group):
+                    pair_in = work.tile([P, 2, QUAD * P * PACK], BF16, align_bytes=64)
+                    live[group]["a_grp"] = pair_in[:, 0, :]
+                    live[group]["pair_in"] = pair_in
+                    live[group - 3]["h_room"] = pair_in[:, 1, :].rearrange("p (k t) -> p k t", t=PACK)
+                else:
+                    a_grp = work.tile([P, QUAD * P * PACK], BF16, align_bytes=64)
+                    live[group]["a_grp"] = a_grp[:]
+            a_grp_words = live[group]["a_grp"].bitcast(F32).rearrange("p (s k u) -> p s k u", s=QUAD, k=P, u=2)
             width = min(2, groups[group][2] - 2 * half)
             copy = nc.vector.tensor_copy if (group, half) in VECTOR_COPIES else nc.scalar.copy
             copy(
@@ -193,8 +210,26 @@ def tile_successiveswintransfomerblock_pb_t_kernel(
                 scales=a_plane[:, :cols],
                 in_=live[group]["a_grp"][:, : PACK * cols],
             )
-            live[group]["a_codes"] = a_codes
-            live[group]["a_plane"] = a_plane
+            live[group]["a_codes"] = a_codes[:]
+            live[group]["a_plane"] = a_plane[:]
+
+        def quantise_both(group):
+            if not joint(group) or ("quantise_both", group) in done:
+                return
+            done.add(("quantise_both", group))
+            done.add(("quantise_attn", group, 0))
+            done.add(("quantise_h", group - 3, 0))
+            pair_codes = work.tile([P, 2 * QUAD * P], U32, align_bytes=64)
+            pair_plane = work.tile([P, 2 * QUAD * P], U8, align_bytes=64)
+            nc.vector.quantize_mx(
+                out=pair_codes[:].bitcast(FP8X4),
+                scales=pair_plane[:],
+                in_=live[group]["pair_in"][:].rearrange("p b k -> p (b k)"),
+            )
+            live[group]["a_codes"] = pair_codes[:, : QUAD * P]
+            live[group]["a_plane"] = pair_plane[:, : QUAD * P]
+            live[group - 3]["h_codes"] = pair_codes[:, QUAD * P :]
+            live[group - 3]["h_plane"] = pair_plane[:, QUAD * P :]
 
         def multiply(codes, plane, s, w_words, w_plane, repeats):
             cols = slice(P * s, P * (s + 1))
@@ -273,6 +308,11 @@ def tile_successiveswintransfomerblock_pb_t_kernel(
             gate = work.tile([P, 32], U8)
             nc.gpsimd.tensor_copy(out=gate[:], in_=live[group]["h_plane"][:, :32])
 
+        def keep_clock(count):
+            attn_t = psum_attn.tile([P, 4 * P], F32)
+            for i in range(count):
+                nc.tensor.matmul(out=attn_t[:], lhsT=ones[:, :P], rhs=ones[:], start=True, stop=True)
+
         def sum_squares(group, slots=range(QUAD)):
             for s in slots:
                 if 0 <= group < len(groups) and s >= groups[group][2]:
@@ -324,6 +364,8 @@ def tile_successiveswintransfomerblock_pb_t_kernel(
             tiles = live[group]
             z_sb = work.tile([P, QUAD, PACK, P], F32)
             for s in range(groups[group][2]):
+                if s in scaled_slots(group):
+                    continue
                 nc.scalar.activation(
                     out=z_sb[:, s].rearrange("r t p -> r p t"),
                     in_=tiles["x"][:, s, :].rearrange("r (p t) -> r p t", t=PACK),
@@ -333,6 +375,55 @@ def tile_successiveswintransfomerblock_pb_t_kernel(
                 )
             tiles["z"] = z_sb
 
+        def scaled_slots(group):
+            return PE_SLOTS if groups[group][2] == QUAD and FIRST_PE <= group < len(groups) - LAST_PE else ()
+
+        def diagonal(group):
+            if not 0 <= group < len(groups) or skip("diagonal", group) or not scaled_slots(group):
+                return
+            diag = work.tile([P, len(PE_SLOTS), P], F32)
+            for i, s in enumerate(PE_SLOTS):
+                if DIAG_ENGINE == "scalar":
+                    nc.scalar.activation(
+                        out=diag[:, i, :], in_=ident[:], func=ACT.Copy, scale=live[group]["rstd"][:, s : s + 1]
+                    )
+                else:
+                    nc.gpsimd.tensor_scalar(
+                        out=diag[:, i, :],
+                        in0=ident[:],
+                        scalar1=live[group]["rstd"][:, s : s + 1],
+                        scalar2=0.0,
+                        op0=MULT,
+                        op1=ADD,
+                    )
+            live[group]["diag"] = diag
+
+        def scale_z(group, banks):
+            if not 0 <= group < len(groups) or not scaled_slots(group):
+                return
+            banks = [bank for bank in banks if not skip("scale_z", group, bank)]
+            for bank in banks:
+                z_t = psum_z.tile([P, 4 * P], F32)
+                live[group]["z_t%d" % bank] = z_t
+            for i, s in enumerate(PE_SLOTS):
+                for bank in banks:
+                    nc.tensor.matmul(
+                        out=live[group]["z_t%d" % bank][:, P * s : P * (s + 1)],
+                        lhsT=live[group]["x"][:, s, bank::PACK],
+                        rhs=live[group]["diag"][:, i, :],
+                        start=True,
+                        stop=False,
+                    )
+                for bank in banks:
+                    nc.tensor.matmul(
+                        out=live[group]["z_t%d" % bank][:, P * s : P * (s + 1)],
+                        lhsT=live[group]["shift"][:, s : s + 1].to_broadcast([P, P]),
+                        rhs=ident[:],
+                        is_transpose=True,
+                        start=False,
+                        stop=True,
+                    )
+
         def transpose_z(group, banks):
             for bank in banks:
                 if skip("transpose_z", group, bank):
@@ -341,13 +432,18 @@ def tile_successiveswintransfomerblock_pb_t_kernel(
                 fit = QUAD // n
                 if bank * fit >= PACK:
                     continue
-                if TAIL and group == len(groups) - 1 and bank == 3:
+                scale_z(group, (bank,))
+                if scaled_slots(group):
+                    z_t = live[group]["z_t%d" % bank]
+                elif TAIL and group == len(groups) - 1 and bank == 3:
                     z_t = psum_attn.tile([P, 4 * P], F32, name="attn_t")
                 else:
                     z_t = psum_z.tile([P, 4 * P], F32)
                 view = z_t[:].rearrange("p (i s k) -> p i s k", i=fit, k=P)
                 for i in range(fit):
                     for s in range(n):
+                        if s in scaled_slots(group):
+                            continue
                         nc.tensor.transpose(view[:, i, s, :], live[group]["z"][:, s, bank * fit + i, :], ident[:])
                 live[group]["z_t%d" % bank] = z_t
 
@@ -388,23 +484,41 @@ def tile_successiveswintransfomerblock_pb_t_kernel(
         def interleave_scalar(group):
             if skip("interleave_scalar", group):
                 return
-            h_grp = work.tile([P, QUAD * P, PACK], BF16, align_bytes=64)
+            if joint(group + 3):
+                h_room = live[group]["h_room"]
+            else:
+                h_grp = work.tile([P, QUAD * P, PACK], BF16, align_bytes=64)
+                h_room = h_grp[:]
             share = scalar_share(group)
-            live[group]["h_grp"] = h_grp
+            live[group]["h_grp"] = h_room
             if group == len(groups) - 1 and TAIL:
                 cols = groups[group][2] * P
                 nc.scalar.copy(
-                    out=h_grp[:, cols // 2 : cols, :].rearrange("p (c i) t -> p c t i", i=4),
+                    out=h_room[:, cols // 2 : cols, :].rearrange("p (c i) t -> p c t i", i=4),
                     in_=live[group]["h_planes"][:, :, cols // 2 : cols].rearrange("p t (c i) -> p c t i", i=4),
                 )
                 return
             if share == 0:
                 return
             nc.scalar.copy(
-                out=h_grp[:, :share, :].rearrange("p (c i) t -> p c t i", i=4),
+                out=h_room[:, :share, :].rearrange("p (c i) t -> p c t i", i=4),
                 in_=live[group]["h_planes"][:, :, :share].rearrange("p t (c i) -> p c t i", i=4),
             )
-            live[group]["h_grp"] = h_grp
+
+        def interleave_gpsimd(group):
+            n = groups[group][2] if 0 <= group < len(groups) else 0
+            if n < QUAD or G_COLS == 0 or group >= len(groups) - 1 or group < FIRST_G or skip("interleave_gpsimd", group):
+                return
+            share = scalar_share(group)
+            nc.gpsimd.tensor_scalar(
+                out=live[group]["h_grp"][:, share : share + G_COLS, :],
+                in0=live[group]["h_planes"][:, :, share : share + G_COLS].rearrange("p t k -> p k t"),
+                scalar1=1.0,
+                scalar2=0.0,
+                op0=MULT,
+                op1=ADD,
+            )
+            live[group]["g_cols"] = G_COLS
 
         def interleave_vector(group):
             if skip("interleave_vector", group):
@@ -415,6 +529,7 @@ def tile_successiveswintransfomerblock_pb_t_kernel(
                 return
             if group == len(groups) - 1 and TAIL:
                 share, cols = 0, cols // 2
+            share += live[group].get("g_cols", 0)
             nc.vector.tensor_copy(
                 out=live[group]["h_grp"][:, share:cols, :],
                 in_=live[group]["h_planes"][:, :, share:cols].rearrange("p t k -> p k t"),
@@ -427,8 +542,8 @@ def tile_successiveswintransfomerblock_pb_t_kernel(
             if half == 0:
                 h_codes = work.tile([P, QUAD * P], U32, align_bytes=64)
                 h_plane = work.tile([P, QUAD * P], U8, align_bytes=64)
-                live[group]["h_codes"] = h_codes
-                live[group]["h_plane"] = h_plane
+                live[group]["h_codes"] = h_codes[:]
+                live[group]["h_plane"] = h_plane[:]
             cols = groups[group][2] * P
             width = cols // 2 if last else cols
             lo = half * width
@@ -585,6 +700,9 @@ def tile_successiveswintransfomerblock_pb_t_kernel(
             load_attn(k + 4)
             load_xm(k + 3)
             interleave_vector(k - 2)
+            if joint(k + 1):
+                project(k, (0,))
+                quantise_both(k + 1)
             quantise_attn(k + 1)
             quantise_h(k - 2)
             quantise_h(k - 2, 1)
@@ -592,12 +710,15 @@ def tile_successiveswintransfomerblock_pb_t_kernel(
             negative_mean(k, 0)
             add_bo2_pairs(k + 1) if PAIR else add_bo2(k + 1)
             project(k, (1, 2))
+            scale_z(k - 1, (0, 1, 2))
             add_bl(k - 1, 0)
             project(k, (3,))
             negative_mean(k, 1)
             copy_attn(k + 2, 0)
             sum_squares(k, (0, 1, 2))
             if k >= len(groups):
+                if k == len(groups) and TAIL_WARM:
+                    keep_clock(TAIL_WARM)
                 linear(k - 2, (0, 1))
             transpose_z(k - 1, (0, 1))
             linear(k - 2, (0, 1))
@@ -614,6 +735,11 @@ def tile_successiveswintransfomerblock_pb_t_kernel(
             linear(k - 2, (3,))
             gain_and_bias(k - 1, (3,))
             copy_attn(k + 2, 1)
+            diagonal(k)
             interleave_scalar(k - 1)
+            interleave_gpsimd(k - 1)
+            if joint(k + 2):
+                interleave_vector(k - 1)
+                project(k + 1, (0,))
             transpose_attn(k + 3, 0)
             normalise(k)

from contextlib import ExitStack

import concourse.mybir as mybir
from concourse.masks import make_identity

FLOPS = 2 * 2 * 8192 * 512 * 512

BF16 = mybir.dt.bfloat16
F32 = mybir.dt.float32
I32 = mybir.dt.int32
U32 = mybir.dt.uint32
U8 = mybir.dt.uint8
FP8X4 = mybir.dt.float8_e4m3fn_x4
ADD = mybir.AluOpType.add
MULT = mybir.AluOpType.mult
ACT = mybir.ActivationFunctionType

P = 128
D = 512
PACK = 4
SIDE = 64
WINDOW = 8
SHIFT = 4
QUAD = 4
QUADS = SIDE // QUAD
LN_EPS = 1e-5
SIZES = (2, 2) + (4,) * 15
WARM = 0
HEAD_WARM = 0
WARM2 = 0
REP_D = {}
REP_K = {}
PAIR = False
TAIL = True
JOINT = True
PE_SLOTS = ()
FIRST_PE = 3
LAST_PE = 1
DIAG_ENGINE = "scalar"
G_COLS = 0
FIRST_G = 2
TAIL_WARM = 0
VECTOR_COPIES = ()
VECTOR_PLANES = ()
SHARES = {}
VECTOR_GROUPS = 2
EARLY = 2


def load_words(nc, pool, words, label):
    w_words = pool.tile([P, D], U32, name=label + "_words", align_bytes=64)
    nc.sync.dma_start(out=w_words[:].bitcast(I32), in_=words.rearrange("o p n t -> (o p) (n t)").bitcast(I32))
    return w_words


def load_scales(nc, w_plane, scales):
    for quadrant in range(4):
        nc.sync.dma_start(
            out=w_plane[32 * quadrant : 32 * quadrant + 4, :].bitcast(I32),
            in_=scales[0, 4 * quadrant : 4 * quadrant + 4, :].bitcast(I32),
        )


def tile_successiveswintransfomerblock_pb_t_kernel(
    tc, attn_win, x_mid, Wo2_words, Wo2_scales, bo2, g4, b4, Wl_words, Wl_scales, bl, out
):
    nc = tc.nc
    attn_quads = attn_win.rearrange(
        "(g wc) (i jh s) d -> wc jh g i (s d)", wc=WINDOW, i=WINDOW, jh=WINDOW // QUAD, s=QUAD
    )
    x_mid_quads = x_mid.rearrange("b (r m s) d -> m (b r) (s d)", r=SIDE, m=QUADS, s=QUAD)
    out_quads = out.rearrange("b (r m s) d -> m (b r) (s d)", r=SIDE, m=QUADS, s=QUAD)

    with ExitStack() as ctx:
        const = ctx.enter_context(tc.tile_pool(name="const", bufs=1))
        loads = ctx.enter_context(tc.tile_pool(name="loads", bufs=4))
        work = ctx.enter_context(tc.tile_pool(name="work", bufs=2))
        long_lived = ctx.enter_context(tc.tile_pool(name="long_lived", bufs=3))
        stores = ctx.enter_context(tc.tile_pool(name="stores", bufs=4))
        psum_attn = ctx.enter_context(tc.psum_pool(name="psum_attn", bufs=1))
        psum_z = ctx.enter_context(tc.psum_pool(name="psum_z", bufs=3))
        psum_mx = ctx.enter_context(tc.psum_pool(name="psum_mx", bufs=3))
        psum_const = ctx.enter_context(tc.psum_pool(name="psum_const", bufs=1))
        ctx.enter_context(tc.manual_schedule())

        groups = []
        taken = 0
        for size in SIZES:
            groups.append((taken // QUAD, taken % QUAD, size))
            taken += size
        live = [{} for _ in groups]
        done = set()

        def joint(group):
            return JOINT and 5 <= group < len(groups)

        def skip(name, group, part=0):
            if not 0 <= group < len(groups) or (name, group, part) in done:
                return True
            done.add((name, group, part))
            return False

        def load_attn(group, half=None):
            if half is None and skip("load_attn", group):
                return
            quad, first, size = groups[group]
            if half is None or half == 0:
                attn_sb = loads.tile([P, QUAD * D], BF16)
                live[group]["attn"] = attn_sb
            lo, hi = (0, size) if half is None else (2 * half, 2 * half + 2)
            if half == 1:
                done.add(("load_attn", group, 0))
            nc.sync.dma_start(
                out=live[group]["attn"][:, D * lo : D * hi],
                in_=attn_quads[quad // 2, quad % 2][:, :, D * (first + lo) : D * (first + hi)],
            )

        def load_xm(group, queue=nc.sync):
            if skip("load_xm", group):
                return
            quad, first, size = groups[group]
            xm_sb = loads.tile([P, QUAD, D], BF16)
            queue.dma_start(
                out=xm_sb[:, :size].rearrange("p s d -> p (s d)"),
                in_=x_mid_quads[(quad - 1) % QUADS][:, D * first : D * (first + size)],
            )
            live[group]["xm"] = xm_sb

        def add_bo2(group, slots=range(QUAD)):
            for s in slots:
                if 0 <= group < len(groups) and s >= groups[group][2]:
                    continue
                if skip("add_bo2", group, s):
                    continue
                if s == 0:
                    c_sb = long_lived.tile([P, QUAD, D], F32)
                    live[group]["c"] = c_sb
                if group < VECTOR_GROUPS:
                    nc.vector.tensor_tensor(
                        out=live[group]["c"][:, s, :], in0=bo2_bank[:], in1=live[group]["xm"][:, s, :], op=ADD
                    )
                else:
                    nc.gpsimd.tensor_tensor(
                        out=live[group]["c"][:, s, :], in0=live[group]["xm"][:, s, :], in1=bo2_rows[:], op=ADD
                    )

        def add_bo2_pairs(group):
            for h in range(2):
                if not 0 <= group < len(groups) or 2 * h >= groups[group][2]:
                    continue
                if ("add_bo2", group, 2 * h) in done:
                    add_bo2(group, (2 * h, 2 * h + 1))
                    continue
                n2 = min(2, groups[group][2] - 2 * h)
                for s in range(2 * h, 2 * h + n2):
                    done.add(("add_bo2", group, s))
                if h == 0:
                    c_sb = long_lived.tile([P, QUAD, D], F32)
                    live[group]["c"] = c_sb
                nc.gpsimd.tensor_tensor(
                    out=live[group]["c"][:, 2 * h : 2 * h + n2, :],
                    in0=live[group]["xm"][:, 2 * h : 2 * h + n2, :],
                    in1=bo2_rows[:].unsqueeze(1).to_broadcast([P, n2, D]),
                    op=ADD,
                )

        def transpose_attn(group, half):
            if skip("transpose_attn", group, half) or 2 * half >= groups[group][2]:
                return
            attn_words = live[group]["attn"][:].bitcast(F32)
            if (group, half) in ((1, 0), (2, 0), (2, 1))[:EARLY]:
                attn_t = psum_z.tile([P, 4 * P], F32, name="z_t")
            else:
                attn_t = psum_attn.tile([P, 4 * P], F32)
            view = attn_t[:].rearrange("p (s u k) -> p s u k", s=2, u=2)
            for s2 in range(min(2, groups[group][2] - 2 * half)):
                s = 2 * half + s2
                for u in range(2):
                    nc.tensor.transpose(view[:, s2, u, :], attn_words[:, 256 * s + u : 256 * (s + 1) : 2], rot[:])
            live[group]["attn_t%d" % half] = view

        def copy_attn(group, half):
            if skip("copy_attn", group, half) or 2 * half >= groups[group][2]:
                return
            if half == 0:
                if joint(group):
                    pair_in = work.tile([P, 2, QUAD * P * PACK], BF16, align_bytes=64)
                    live[group]["a_grp"] = pair_in[:, 0, :]
                    live[group]["pair_in"] = pair_in
                    live[group - 3]["h_room"] = pair_in[:, 1, :].rearrange("p (k t) -> p k t", t=PACK)
                else:
                    a_grp = work.tile([P, QUAD * P * PACK], BF16, align_bytes=64)
                    live[group]["a_grp"] = a_grp[:]
            a_grp_words = live[group]["a_grp"].bitcast(F32).rearrange("p (s k u) -> p s k u", s=QUAD, k=P, u=2)
            width = min(2, groups[group][2] - 2 * half)
            copy = nc.vector.tensor_copy if (group, half) in VECTOR_COPIES else nc.scalar.copy
            copy(
                out=a_grp_words[:, 2 * half : 2 * half + width],
                in_=live[group]["attn_t%d" % half][:, :width].rearrange("p s u k -> p s k u"),
            )

        def quantise_attn(group):
            if skip("quantise_attn", group):
                return
            a_codes = work.tile([P, QUAD * P], U32, align_bytes=64)
            a_plane = work.tile([P, QUAD * P], U8, align_bytes=64)
            cols = groups[group][2] * P
            nc.vector.quantize_mx(
                out=a_codes[:, :cols].bitcast(FP8X4),
                scales=a_plane[:, :cols],
                in_=live[group]["a_grp"][:, : PACK * cols],
            )
            live[group]["a_codes"] = a_codes[:]
            live[group]["a_plane"] = a_plane[:]

        def quantise_both(group):
            if not joint(group) or ("quantise_both", group) in done:
                return
            done.add(("quantise_both", group))
            done.add(("quantise_attn", group, 0))
            done.add(("quantise_h", group - 3, 0))
            pair_codes = work.tile([P, 2 * QUAD * P], U32, align_bytes=64)
            pair_plane = work.tile([P, 2 * QUAD * P], U8, align_bytes=64)
            nc.vector.quantize_mx(
                out=pair_codes[:].bitcast(FP8X4),
                scales=pair_plane[:],
                in_=live[group]["pair_in"][:].rearrange("p b k -> p (b k)"),
            )
            live[group]["a_codes"] = pair_codes[:, : QUAD * P]
            live[group]["a_plane"] = pair_plane[:, : QUAD * P]
            live[group - 3]["h_codes"] = pair_codes[:, QUAD * P :]
            live[group - 3]["h_plane"] = pair_plane[:, QUAD * P :]

        def multiply(codes, plane, s, w_words, w_plane, repeats):
            cols = slice(P * s, P * (s + 1))
            acc = psum_mx.tile([P, D], F32)
            for repeat in range(repeats):
                nc.tensor.matmul_mx(
                    out=acc[:],
                    lhsT=codes[:, cols].bitcast(FP8X4),
                    lhsT_scale=plane[:, cols],
                    rhs=w_words[:].bitcast(FP8X4),
                    rhs_scale=w_plane[:],
                    start=True,
                    stop=True,
                )
            return acc

        def project(group, slots=range(QUAD)):
            for s in slots:
                if 0 <= group < len(groups) and s >= groups[group][2]:
                    continue
                if skip("project", group, s):
                    continue
                tiles = live[group]
                if s == 0:
                    x_sb = work.tile([P, QUAD, D], F32)
                    row_sum = long_lived.tile([P, QUAD], F32)
                    tiles["x"] = x_sb
                    tiles["row_sum"] = row_sum
                acc = multiply(tiles["a_codes"], tiles["a_plane"], s, wo_words, wo_plane, REP_D.get(s, 1))
                nc.vector.scalar_tensor_tensor(
                    out=tiles["x"][:, s, :],
                    in0=acc[:],
                    scalar=1.0,
                    in1=tiles["c"][:, s, :],
                    op0=MULT,
                    op1=ADD,
                    accum_out=tiles["row_sum"][:, s : s + 1],
                )

        def negative_mean(group, part):
            if skip("negative_mean", group, part):
                return
            lo, hi = ((0, 1), (1, groups[group][2]))[part]
            if lo == hi:
                return
            if part == 0:
                neg_mean = long_lived.tile([P, QUAD], F32)
                live[group]["neg_mean"] = neg_mean
            nc.gpsimd.tensor_scalar(
                out=live[group]["neg_mean"][:, lo:hi],
                in0=live[group]["row_sum"][:, lo:hi],
                scalar1=-1.0 / D,
                scalar2=None,
                op0=MULT,
            )

        def add_bl(group, half):
            if skip("add_bl", group, half):
                return
            n = groups[group][2]
            lo, hi = half * n // 2, (half + 1) * n // 2
            if half == 0:
                xb_sb = long_lived.tile([P, QUAD, D], F32)
                live[group]["xb"] = xb_sb
            nc.vector.tensor_tensor(
                out=live[group]["xb"][:, lo:hi],
                in0=live[group]["x"][:, lo:hi],
                in1=bl_bank[:].unsqueeze(1).to_broadcast([P, hi - lo, D]),
                op=ADD,
            )

        def leave_port(group):
            if not 3 <= group < len(groups) - 3 or ("leave_port", group) in done:
                return
            done.add(("leave_port", group))
            gate = work.tile([P, 32], U8)
            nc.gpsimd.tensor_copy(out=gate[:], in_=live[group]["h_plane"][:, :32])

        def keep_clock(count):
            attn_t = psum_attn.tile([P, 4 * P], F32)
            for i in range(count):
                nc.tensor.matmul(out=attn_t[:], lhsT=ones[:, :P], rhs=ones[:], start=True, stop=True)

        def sum_squares(group, slots=range(QUAD)):
            for s in slots:
                if 0 <= group < len(groups) and s >= groups[group][2]:
                    continue
                if skip("sum_squares", group, s):
                    continue
                tiles = live[group]
                n = groups[group][2]
                if s == 0:
                    sq_sum = long_lived.tile([P, QUAD], F32)
                    tiles["sq_sum"] = sq_sum
                squares = work.tile([P, D], BF16)
                nc.scalar.activation(
                    out=squares[:],
                    in_=tiles["x"][:, s, :],
                    func=ACT.Square,
                    bias=tiles["row_sum"][:, s : s + 1],
                    scale=-float(D),
                    accum_out=tiles["sq_sum"][:, s : s + 1],
                )

        def inverse_std(group):
            if skip("inverse_std", group):
                return
            n = groups[group][2]
            rstd = long_lived.tile([P, QUAD], F32)
            nc.scalar.activation(
                out=rstd[:, :n],
                in_=live[group]["sq_sum"][:, :n],
                func=ACT.Abs_reciprocal_sqrt,
                bias=eps_col[:],
                scale=1.0 / D**3,
            )
            live[group]["rstd"] = rstd

        def mean_over_std(group):
            if skip("mean_over_std", group):
                return
            n = groups[group][2]
            shift = long_lived.tile([P, QUAD], F32)
            nc.gpsimd.tensor_tensor(
                out=shift[:, :n], in0=live[group]["neg_mean"][:, :n], in1=live[group]["rstd"][:, :n], op=MULT
            )
            live[group]["shift"] = shift

        def normalise(group):
            if skip("normalise", group):
                return
            tiles = live[group]
            z_sb = work.tile([P, QUAD, PACK, P], F32)
            for s in range(groups[group][2]):
                if s in scaled_slots(group):
                    continue
                nc.scalar.activation(
                    out=z_sb[:, s].rearrange("r t p -> r p t"),
                    in_=tiles["x"][:, s, :].rearrange("r (p t) -> r p t", t=PACK),
                    func=ACT.Identity,
                    bias=tiles["shift"][:, s : s + 1],
                    scale=tiles["rstd"][:, s : s + 1],
                )
            tiles["z"] = z_sb

        def scaled_slots(group):
            return PE_SLOTS if groups[group][2] == QUAD and FIRST_PE <= group < len(groups) - LAST_PE else ()

        def diagonal(group):
            if not 0 <= group < len(groups) or skip("diagonal", group) or not scaled_slots(group):
                return
            diag = work.tile([P, len(PE_SLOTS), P], F32)
            for i, s in enumerate(PE_SLOTS):
                if DIAG_ENGINE == "scalar":
                    nc.scalar.activation(
                        out=diag[:, i, :], in_=ident[:], func=ACT.Copy, scale=live[group]["rstd"][:, s : s + 1]
                    )
                else:
                    nc.gpsimd.tensor_scalar(
                        out=diag[:, i, :],
                        in0=ident[:],
                        scalar1=live[group]["rstd"][:, s : s + 1],
                        scalar2=0.0,
                        op0=MULT,
                        op1=ADD,
                    )
            live[group]["diag"] = diag

        def scale_z(group, banks):
            if not 0 <= group < len(groups) or not scaled_slots(group):
                return
            banks = [bank for bank in banks if not skip("scale_z", group, bank)]
            for bank in banks:
                z_t = psum_z.tile([P, 4 * P], F32)
                live[group]["z_t%d" % bank] = z_t
            for i, s in enumerate(PE_SLOTS):
                for bank in banks:
                    nc.tensor.matmul(
                        out=live[group]["z_t%d" % bank][:, P * s : P * (s + 1)],
                        lhsT=live[group]["x"][:, s, bank::PACK],
                        rhs=live[group]["diag"][:, i, :],
                        start=True,
                        stop=False,
                    )
                for bank in banks:
                    nc.tensor.matmul(
                        out=live[group]["z_t%d" % bank][:, P * s : P * (s + 1)],
                        lhsT=live[group]["shift"][:, s : s + 1].to_broadcast([P, P]),
                        rhs=ident[:],
                        is_transpose=True,
                        start=False,
                        stop=True,
                    )

        def transpose_z(group, banks):
            for bank in banks:
                if skip("transpose_z", group, bank):
                    continue
                n = groups[group][2]
                fit = QUAD // n
                if bank * fit >= PACK:
                    continue
                scale_z(group, (bank,))
                if scaled_slots(group):
                    z_t = live[group]["z_t%d" % bank]
                elif TAIL and group == len(groups) - 1 and bank == 3:
                    z_t = psum_attn.tile([P, 4 * P], F32, name="attn_t")
                else:
                    z_t = psum_z.tile([P, 4 * P], F32)
                view = z_t[:].rearrange("p (i s k) -> p i s k", i=fit, k=P)
                for i in range(fit):
                    for s in range(n):
                        if s in scaled_slots(group):
                            continue
                        nc.tensor.transpose(view[:, i, s, :], live[group]["z"][:, s, bank * fit + i, :], ident[:])
                live[group]["z_t%d" % bank] = z_t

        def gain_and_bias(group, banks):
            for bank in banks:
                if skip("gain_and_bias", group, bank):
                    continue
                n = groups[group][2]
                fit = QUAD // n
                if bank * fit >= PACK:
                    continue
                if bank == 0:
                    h_planes = work.tile([P, PACK, QUAD * P], BF16)
                    live[group]["h_planes"] = h_planes
                for i in range(fit):
                    t = bank * fit + i
                    if (group, t) in VECTOR_PLANES:
                        nc.vector.tensor_scalar(
                            out=live[group]["h_planes"][:, t, : n * P],
                            in0=live[group]["z_t%d" % bank][:, n * P * i : n * P * (i + 1)],
                            scalar1=g_col[:, t : t + 1],
                            scalar2=b_col[:, t : t + 1],
                            op0=MULT,
                            op1=ADD,
                        )
                        continue
                    nc.scalar.activation(
                        out=live[group]["h_planes"][:, t, : n * P],
                        in_=live[group]["z_t%d" % bank][:, n * P * i : n * P * (i + 1)],
                        func=ACT.Identity,
                        bias=b_col[:, t : t + 1],
                        scale=g_col[:, t : t + 1],
                    )

        def scalar_share(group):
            return int(groups[group][2] * P * SHARES.get(group, 0.3125))

        def interleave_scalar(group):
            if skip("interleave_scalar", group):
                return
            if joint(group + 3):
                h_room = live[group]["h_room"]
            else:
                h_grp = work.tile([P, QUAD * P, PACK], BF16, align_bytes=64)
                h_room = h_grp[:]
            share = scalar_share(group)
            live[group]["h_grp"] = h_room
            if group == len(groups) - 1 and TAIL:
                cols = groups[group][2] * P
                nc.scalar.copy(
                    out=h_room[:, cols // 2 : cols, :].rearrange("p (c i) t -> p c t i", i=4),
                    in_=live[group]["h_planes"][:, :, cols // 2 : cols].rearrange("p t (c i) -> p c t i", i=4),
                )
                return
            if share == 0:
                return
            nc.scalar.copy(
                out=h_room[:, :share, :].rearrange("p (c i) t -> p c t i", i=4),
                in_=live[group]["h_planes"][:, :, :share].rearrange("p t (c i) -> p c t i", i=4),
            )

        def interleave_gpsimd(group):
            n = groups[group][2] if 0 <= group < len(groups) else 0
            if n < QUAD or G_COLS == 0 or group >= len(groups) - 1 or group < FIRST_G or skip("interleave_gpsimd", group):
                return
            share = scalar_share(group)
            nc.gpsimd.tensor_scalar(
                out=live[group]["h_grp"][:, share : share + G_COLS, :],
                in0=live[group]["h_planes"][:, :, share : share + G_COLS].rearrange("p t k -> p k t"),
                scalar1=1.0,
                scalar2=0.0,
                op0=MULT,
                op1=ADD,
            )
            live[group]["g_cols"] = G_COLS

        def interleave_vector(group):
            if skip("interleave_vector", group):
                return
            cols = groups[group][2] * P
            share = scalar_share(group)
            if share == cols:
                return
            if group == len(groups) - 1 and TAIL:
                share, cols = 0, cols // 2
            share += live[group].get("g_cols", 0)
            nc.vector.tensor_copy(
                out=live[group]["h_grp"][:, share:cols, :],
                in_=live[group]["h_planes"][:, :, share:cols].rearrange("p t k -> p k t"),
            )

        def quantise_h(group, half=0):
            last = group == len(groups) - 1 and TAIL
            if (half == 1 and not last) or skip("quantise_h", group, half):
                return
            if half == 0:
                h_codes = work.tile([P, QUAD * P], U32, align_bytes=64)
                h_plane = work.tile([P, QUAD * P], U8, align_bytes=64)
                live[group]["h_codes"] = h_codes[:]
                live[group]["h_plane"] = h_plane[:]
            cols = groups[group][2] * P
            width = cols // 2 if last else cols
            lo = half * width
            nc.vector.quantize_mx(
                out=live[group]["h_codes"][:, lo : lo + width].bitcast(FP8X4),
                scales=live[group]["h_plane"][:, lo : lo + width],
                in_=live[group]["h_grp"][:, lo : lo + width].rearrange("p k t -> p (k t)"),
            )

        def linear(group, slots=range(QUAD)):
            for s in slots:
                if 0 <= group < len(groups) and s >= groups[group][2]:
                    continue
                if skip("linear", group, s):
                    continue
                tiles = live[group]
                quad, first, size = groups[group]
                acc = multiply(tiles["h_codes"], tiles["h_plane"], s, wl_words, wl_plane, REP_K.get(s, 1))
                o_sb = stores.tile([P, D], F32)
                nc.vector.tensor_tensor(out=o_sb[:], in0=acc[:], in1=tiles["xb"][:, s, :], op=ADD)
                out_cols = slice(D * (first + s), D * (first + s + 1))
                nc.sync.dma_start(out=out_quads[(quad - 1) % QUADS][:, out_cols], in_=o_sb[:])

        eps_col = const.tile([P, 1], F32)
        nc.vector.memset(eps_col[:], LN_EPS)
        warm = const.tile([P, 1], F32)
        nc.scalar.activation(out=warm[:], in_=eps_col[:], func=ACT.Abs_reciprocal_sqrt, bias=0.0, scale=1.0)
        wo_plane = const.tile([P, D], U8, align_bytes=64)
        wl_plane = const.tile([P, D], U8, align_bytes=64)
        bias_rows = const.tile([P, 2, D], BF16)
        nc.vector.memset(bias_rows[:].rearrange("p b n -> p (b n)").bitcast(I32), 0)
        nc.vector.memset(wo_plane[:].bitcast(I32), 0)
        nc.vector.memset(wl_plane[:].bitcast(I32), 0)
        ident = const.tile([P, P], F32)
        make_identity(nc, ident[:])
        ones = const.tile([P, D], BF16)
        nc.gpsimd.memset(ones[:], 1.0)
        for i in range(HEAD_WARM):
            acc = psum_mx.tile([P, D], F32)
            nc.tensor.matmul(out=acc[:], lhsT=ones[:, :P], rhs=ones[:], start=True, stop=True)
        rot = const.tile([P, P], F32)
        for image in range(P // SIDE):
            lo = SIDE * image
            nc.vector.tensor_copy(out=rot[:, lo : lo + SIDE - SHIFT], in_=ident[:, lo + SHIFT : lo + SIDE])
            nc.vector.tensor_copy(out=rot[:, lo + SIDE - SHIFT : lo + SIDE], in_=ident[:, lo : lo + SHIFT])
        nc.scalar.dma_start(out=bias_rows[0:1, 0, :], in_=bo2.unsqueeze(0))
        load_attn(0)
        load_scales(nc, wo_plane, Wo2_scales)
        load_attn(1)
        load_xm(0)
        wo_words = load_words(nc, const, Wo2_words, "wo")
        load_attn(2, 0)
        load_xm(1)
        load_attn(2, 1)
        load_xm(2)
        nc.sync.dma_start(out=bias_rows[0:1, 1, :], in_=bl.unsqueeze(0))
        g_bf = const.tile([P, PACK], BF16)
        nc.sync.dma_start(out=g_bf[:], in_=g4.rearrange("(p t) -> p t", t=PACK))
        b_bf = const.tile([P, PACK], BF16)
        nc.sync.dma_start(out=b_bf[:], in_=b4.rearrange("(p t) -> p t", t=PACK))
        load_attn(3)
        load_xm(3)
        wl_words = load_words(nc, const, Wl_words, "wl")
        load_scales(nc, wl_plane, Wl_scales)
        transpose_attn(0, 0)
        bo2_bank = psum_z.tile([P, D], F32, name="z_t")
        nc.tensor.matmul(out=bo2_bank[:], lhsT=ones[:, :P], rhs=bias_rows[:, 0, :], start=True, stop=True)
        copy_attn(0, 0)
        bo2_rows = const.tile([P, D], F32)
        nc.scalar.copy(out=bo2_rows[:], in_=bo2_bank[:])
        transpose_attn(1, 0)
        copy_attn(1, 0)
        quantise_attn(0)
        add_bo2(0)
        quantise_attn(1)
        project(0)
        transpose_attn(2, 0)
        copy_attn(2, 0)
        add_bo2(1)
        load_attn(4)
        load_xm(4)
        sum_squares(0)
        negative_mean(0, 0)
        negative_mean(0, 1)
        project(1)
        transpose_attn(2, 1)
        copy_attn(2, 1)
        bl_bank = psum_const.tile([P, D], F32)
        nc.tensor.matmul(out=bl_bank[:], lhsT=ones[:, :P], rhs=bias_rows[:, 1, :], start=True, stop=True)
        add_bo2(2, (0,))
        inverse_std(0)
        mean_over_std(0)
        add_bo2(2, (1,))
        quantise_attn(2)
        g_col = const.tile([P, PACK], F32)
        nc.vector.tensor_copy(out=g_col[:], in_=g_bf[:])
        b_col = const.tile([P, PACK], F32)
        nc.vector.tensor_copy(out=b_col[:], in_=b_bf[:])
        sum_squares(1)
        transpose_attn(3, 0)
        normalise(0)
        negative_mean(1, 0)
        negative_mean(1, 1)
        inverse_std(1)
        mean_over_std(1)
        add_bo2(2, (2, 3))
        add_bl(0, 0)
        add_bl(0, 1)
        project(2, (0, 1))
        transpose_z(0, (0, 1, 2))
        copy_attn(3, 0)
        add_bo2(3, (0, 1))
        gain_and_bias(0, (0, 1, 2, 3))
        interleave_scalar(0)
        add_bl(1, 0)
        add_bl(1, 1)
        project(2, (2, 3))
        transpose_attn(3, 1)
        normalise(1)
        copy_attn(3, 1)
        interleave_vector(0)
        quantise_attn(3)
        quantise_h(0)
        negative_mean(2, 0)
        negative_mean(2, 1)
        add_bo2(3, (2, 3))
        sum_squares(2)
        inverse_std(2)
        mean_over_std(2)
        load_attn(5)
        load_xm(5)
        transpose_z(1, (0, 1, 2))
        project(3, (0, 1))
        transpose_attn(4, 0)
        linear(0)
        gain_and_bias(1, (0, 1, 2, 3))
        interleave_scalar(1)
        copy_attn(4, 0)
        normalise(2)
        transpose_attn(4, 1)
        copy_attn(4, 1)
        add_bl(2, 0)
        project(3, (2, 3))
        transpose_attn(5, 0)
        sum_squares(3, (0, 1, 2))
        interleave_vector(1)
        quantise_attn(4)
        quantise_h(1)
        add_bl(2, 1)
        load_attn(6)
        load_xm(6)

        for k in range(-3, len(groups) + 2):
            load_attn(k + 4)
            load_xm(k + 3)
            interleave_vector(k - 2)
            if joint(k + 1):
                project(k, (0,))
                quantise_both(k + 1)
            quantise_attn(k + 1)
            quantise_h(k - 2)
            quantise_h(k - 2, 1)
            project(k, (0,))
            negative_mean(k, 0)
            add_bo2_pairs(k + 1) if PAIR else add_bo2(k + 1)
            project(k, (1, 2))
            scale_z(k - 1, (0, 1, 2))
            add_bl(k - 1, 0)
            project(k, (3,))
            negative_mean(k, 1)
            copy_attn(k + 2, 0)
            sum_squares(k, (0, 1, 2))
            if k >= len(groups):
                if k == len(groups) and TAIL_WARM:
                    keep_clock(TAIL_WARM)
                linear(k - 2, (0, 1))
            transpose_z(k - 1, (0, 1))
            linear(k - 2, (0, 1))
            transpose_z(k - 1, (2,) if k < len(groups) else (2, 3))
            add_bl(k - 1, 1)
            gain_and_bias(k - 1, (0, 1))
            sum_squares(k, (3,))
            gain_and_bias(k - 1, (2,))
            inverse_std(k)
            mean_over_std(k)
            linear(k - 2, (2,))
            transpose_z(k - 1, (3,))
            transpose_attn(k + 2, 1)
            linear(k - 2, (3,))
            gain_and_bias(k - 1, (3,))
            copy_attn(k + 2, 1)
            diagonal(k)
            interleave_scalar(k - 1)
            interleave_gpsimd(k - 1)
            if joint(k + 2):
                interleave_vector(k - 1)
                project(k + 1, (0,))
            transpose_attn(k + 3, 0)
            normalise(k)
